import numpy as np
import ml_dtypes


def mxq(x, axis, fmt="e4m3"):
    dtype, down = {"e4m3": (ml_dtypes.float8_e4m3fn, 7), "e5m2": (ml_dtypes.float8_e5m2, 14)}[fmt]
    v = np.moveaxis(np.asarray(x, np.float32).astype(ml_dtypes.bfloat16).astype(np.float64), axis, -1)
    blocks = v.reshape(v.shape[:-1] + (-1, 32))
    amax = np.abs(blocks).max(-1, keepdims=True)
    byte = np.maximum(np.where(amax > 0, np.frexp(amax)[1] - 1 + 127, 0) - down, 1)
    scale = np.exp2(byte - 127.0)
    codes = (blocks / scale).astype(np.float32).astype(dtype).astype(np.float64)
    return np.moveaxis((codes * scale).reshape(v.shape), -1, axis)


WIDE = False


def mx_kscale(k):
    if not WIDE:
        return np.ones(k)
    levels = np.array([10, -10, 5, -5, 0])
    a = np.random.permutation(np.resize(levels, k // 512 * 4)).reshape(k // 512, 4)
    idx = np.arange(k)
    return np.exp2(a[idx // 512, idx % 128 // 32])


BF16 = ml_dtypes.bfloat16


def bf(x):
    return np.asarray(x, np.float32).astype(BF16)


def f64(x):
    return np.asarray(x).astype(np.float64)


B, S, DIM, QL, KVL, H, DN, DR, DV, P0 = 1, 128, 1024, 512, 512, 16, 64, 64, 128, 37
EPS = 1e-6
HALF = DR // 2


def rms_norm(v, w):
    return v / np.sqrt(np.mean(v * v, axis=-1, keepdims=True) + EPS) * w


def rope(v, start):
    theta = 10000.0 ** (-np.arange(HALF) / HALF)
    pos = np.arange(v.shape[-2]) + start
    ang = pos[:, None] * theta[None, :]
    ang2 = np.concatenate([ang, ang], axis=-1)
    v1, v2 = v[..., :HALF], v[..., HALF:]
    rot = np.concatenate([-v2, v1], axis=-1)
    return v * np.cos(ang2) + rot * np.sin(ang2)


def setup_inputs():
    s, t = mx_kscale(DIM), mx_kscale(QL)
    return {"x": bf(np.random.standard_normal((B, S, DIM)) * s),
            "wq_a": bf(np.random.standard_normal((DIM, QL)) / np.sqrt(DIM) / s[:, None]),
            "q_norm_w": bf((1.0 + 0.1 * np.random.standard_normal(QL)) * t),
            "wq_b": bf(np.random.standard_normal((QL, H * (DN + DR))) / np.sqrt(QL) / t[:, None])}


def reference(x, wq_a, q_norm_w, wq_b):
    c = mxq(f64(x), 2, "e4m3") @ mxq(f64(wq_a), 0, "e4m3")
    cn = rms_norm(c, f64(q_norm_w))
    q = (mxq(cn, 2, "e4m3") @ mxq(f64(wq_b), 0, "e4m3")).reshape(B, S, H, DN + DR)
    q_nope, q_rope = q[..., :DN], q[..., DN:]
    q_rope = rope(q_rope.reshape(B, H, S, DR), P0).reshape(B, S, H, DR)
    return np.concatenate([q_nope, q_rope], axis=-1)

@@ -1,0 +1,241 @@
+import math
+from contextlib import ExitStack
+
+import concourse.mybir as mybir
+from concourse.masks import make_identity
+
+F32 = mybir.dt.float32
+BF16 = mybir.dt.bfloat16
+I32 = mybir.dt.int32
+U32 = mybir.dt.uint32
+U8 = mybir.dt.uint8
+FP8X4 = mybir.dt.float8_e4m3fn_x4
+ALU = mybir.AluOpType
+ACT = mybir.ActivationFunctionType
+
+P = 128
+PACK = 4
+K_PASS = P * PACK
+DIM = 1024
+QL = 512
+HEADS = 16
+HEAD = 128
+NOPE = 64
+HALF = 32
+FIRST_POSITION = 37
+EPS = 1e-6
+N_TILE = 512
+TILE_HEADS = N_TILE // HEAD
+A_PASSES = DIM // K_PASS
+B_TILES = HEADS * HEAD // N_TILE
+RUN = 4
+A_VECTOR_COLS = 320
+FIRST_PIECE = 128
+
+FLOPS = 2 * P * DIM * QL + 2 * P * QL * HEADS * HEAD
+
+
+def regroup(copy, grouped, raw, lo, hi):
+    copy(
+        out=grouped[:, PACK * lo : PACK * hi].rearrange("p (c i t) -> p c t i", i=RUN, t=PACK),
+        in_=raw[:, :, lo:hi].rearrange("p t (c i) -> p c t i", i=RUN),
+    )
+
+
+def tile_mla_pa_s_kernel(tc, x, wq_a, q_norm_w, wq_b, out):
+    nc = tc.nc
+    with ExitStack() as ctx:
+        keep = ctx.enter_context(tc.tile_pool(name="keep", bufs=1))
+        work = ctx.enter_context(tc.tile_pool(name="work", bufs=2))
+        psum = ctx.enter_context(tc.psum_pool(name="psum", bufs=1))
+        q_psum = ctx.enter_context(tc.psum_pool(name="q_psum", bufs=B_TILES))
+        ctx.enter_context(tc.manual_schedule())
+
+        x_sb = keep.tile([P, DIM], BF16)
+        raw_a = [keep.tile([P, PACK, QL], BF16, name="raw_a%d" % g) for g in range(A_PASSES)]
+
+        def load_a(g):
+            nc.sync.dma_start(
+                out=raw_a[g][:].rearrange("q (u e) c -> q u e c", u=2),
+                in_=wq_a[K_PASS * g : K_PASS * (g + 1), :].rearrange(
+                    "(u q e) c -> q u e c", u=2, e=2
+                ),
+            )
+
+        load_a(0)
+        nc.sync.dma_start(out=x_sb[:], in_=x.rearrange("b s k -> (b s) k"))
+        load_a(1)
+        raw_b = [keep.tile([P, PACK, N_TILE], BF16, name="raw_b%d" % n) for n in range(B_TILES)]
+        for n in range(B_TILES):
+            nc.sync.dma_start(
+                out=raw_b[n][:],
+                in_=wq_b[:, N_TILE * n : N_TILE * (n + 1)].rearrange("(t p) c -> p t c", p=P),
+            )
+        gain = keep.tile([P, PACK], BF16)
+        with nc.allow_non_contiguous_dma(reason="512 gains, one to a partition and value"):
+            nc.scalar.dma_start(out=gain[:], in_=q_norm_w.rearrange("(t p) -> p t", p=P))
+
+        position_i = keep.tile([P, HEADS], I32)
+        nc.gpsimd.iota(position_i[:], pattern=[[1, HEADS]], base=0, channel_multiplier=HEADS)
+        minus_half = keep.tile([P, 1], F32)
+        nc.gpsimd.memset(minus_half[:], -0.5)
+        ident = keep.tile([P, P], F32)
+        make_identity(nc, ident[:])
+        warm = keep.tile([P, 1], F32)
+        nc.scalar.activation(out=warm[:], in_=minus_half[:], func=ACT.Sin)
+
+        theta_1 = 10000.0 ** (-1.0 / HALF)
+        theta = keep.tile([P, HALF], F32)
+        nc.vector.memset(theta[:, 0:1], 1.0)
+        w = 1
+        while w < HALF:
+            nc.vector.tensor_scalar_mul(
+                out=theta[:, w : 2 * w], in0=theta[:, 0:w], scalar1=theta_1**w
+            )
+            w *= 2
+        nc.vector.tensor_single_scalar(
+            out=position_i[:], in_=position_i[:], scalar=P - 1, op=ALU.bitwise_and
+        )
+        position = keep.tile([P, HEADS], F32)
+        nc.vector.tensor_scalar(
+            out=position[:], in0=position_i[:], scalar1=FIRST_POSITION, scalar2=1.0 / (2.0 * math.pi),
+            op0=ALU.add, op1=ALU.mult,
+        )
+        turns = keep.tile([P, 2, HEADS, HALF], F32)
+        nc.vector.tensor_tensor(
+            out=turns[:, 0],
+            in0=position[:].unsqueeze(2).to_broadcast([P, HEADS, HALF]),
+            in1=theta[:].unsqueeze(1).to_broadcast([P, HEADS, HALF]),
+            op=ALU.mult,
+        )
+        nc.vector.tensor_scalar_add(out=turns[:, 1], in0=turns[:, 0], scalar1=0.25)
+        whole = keep.tile([P, 2, HEADS, HALF], I32)
+        nc.vector.tensor_copy(out=whole[:], in_=turns[:])
+        nc.vector.tensor_tensor(out=turns[:], in0=turns[:], in1=whole[:], op=ALU.subtract)
+        sin_cos = keep.tile([P, 2, HEADS, HALF], F32)
+        nc.scalar.activation(out=sin_cos[:], in_=turns[:], func=ACT.Sin, scale=2.0 * math.pi)
+
+        x_words = x_sb[:].bitcast(F32)
+        xt_ps = psum.tile([P, 2 * A_PASSES, P], F32)
+        for v in range(2 * A_PASSES):
+            nc.tensor.transpose(xt_ps[:, v, :], x_words[:, P * v : P * (v + 1)], ident[:])
+        x_grouped = keep.tile([P, A_PASSES * P * PACK], BF16, align_bytes=64)
+        x_codes = keep.tile([P, A_PASSES * P], U32, align_bytes=64)
+        x_scales = keep.tile([P, A_PASSES * P], U8, align_bytes=64)
+
+        a_grouped = keep.tile([P, A_PASSES, PACK * QL], BF16, align_bytes=64)
+        a_codes = keep.tile([P, A_PASSES, QL], U32, align_bytes=64)
+        a_scales = keep.tile([P, A_PASSES, QL], U8, align_bytes=64)
+
+        def quantise_a(g):
+            nc.vector.quantize_mx(
+                out=a_codes[:, g].bitcast(FP8X4), scales=a_scales[:, g], in_=a_grouped[:, g]
+            )
+
+        regroup(nc.vector.tensor_copy, a_grouped[:, 0], raw_a[0], 0, QL)
+        quantise_a(0)
+        nc.scalar.copy(
+            out=x_grouped[:].bitcast(F32).rearrange("q (g s u) -> q g s u", g=A_PASSES, u=2),
+            in_=xt_ps[:].rearrange("q (g u) s -> q g s u", g=A_PASSES),
+        )
+        regroup(nc.vector.tensor_copy, a_grouped[:, 1], raw_a[1], 0, A_VECTOR_COLS)
+        regroup(nc.scalar.copy, a_grouped[:, 1], raw_a[1], A_VECTOR_COLS, QL)
+        nc.vector.quantize_mx(out=x_codes[:].bitcast(FP8X4), scales=x_scales[:], in_=x_grouped[:])
+        quantise_a(1)
+
+        c_ps = psum.tile([P, QL], F32)
+        for g in range(A_PASSES):
+            nc.tensor.matmul_mx(
+                out=c_ps[:],
+                lhsT=x_codes[:, P * g : P * (g + 1)].bitcast(FP8X4),
+                lhsT_scale=x_scales[:, P * g : P * (g + 1)],
+                rhs=a_codes[:, g].bitcast(FP8X4),
+                rhs_scale=a_scales[:, g],
+                start=(g == 0),
+                stop=(g == A_PASSES - 1),
+            )
+
+        b_grouped = keep.tile([P, B_TILES, PACK * N_TILE], BF16, align_bytes=64)
+        b_codes = keep.tile([P, B_TILES, N_TILE], U32, align_bytes=64)
+        b_scales = keep.tile([P, B_TILES, N_TILE], U8, align_bytes=64)
+
+        def quantise_b(n):
+            nc.vector.quantize_mx(
+                out=b_codes[:, n].bitcast(FP8X4), scales=b_scales[:, n], in_=b_grouped[:, n]
+            )
+
+        squares = keep.tile([P, QL], F32)
+        sum_squares = keep.tile([P, 1], F32)
+        nc.scalar.activation(out=squares[:], in_=c_ps[:], func=ACT.Square, accum_out=sum_squares[:])
+        mean_square = keep.tile([P, 1], F32)
+        nc.gpsimd.tensor_scalar(
+            out=mean_square[:], in0=sum_squares[:], scalar1=1.0 / QL, scalar2=EPS,
+            op0=ALU.mult, op1=ALU.add,
+        )
+        inv_rms = keep.tile([P, 1], F32)
+        nc.gpsimd.tensor_tensor(out=inv_rms[:], in0=mean_square[:], in1=minus_half[:], op=ALU.pow)
+        regroup(nc.vector.tensor_copy, b_grouped[:, 0], raw_b[0], 0, N_TILE)
+        quantise_b(0)
+        regroup(nc.scalar.copy, b_grouped[:, 1], raw_b[1], 0, FIRST_PIECE)
+        c_scaled = keep.tile([P, QL], F32)
+        nc.scalar.activation(out=c_scaled[:], in_=c_ps[:], func=ACT.Copy, scale=inv_rms[:, 0:1])
+        ct_ps = psum.tile([P, PACK, P], F32)
+        for t in range(PACK):
+            nc.tensor.transpose(ct_ps[:, t, :], c_scaled[:, P * t : P * (t + 1)], ident[:])
+        regroup(nc.scalar.copy, b_grouped[:, 1], raw_b[1], FIRST_PIECE, N_TILE)
+        regroup(nc.vector.tensor_copy, b_grouped[:, 2], raw_b[2], 0, N_TILE)
+        quantise_b(2)
+        regroup(nc.scalar.copy, b_grouped[:, 3], raw_b[3], 0, N_TILE)
+        cn_grouped = keep.tile([P, P, PACK], BF16, align_bytes=64)
+        nc.vector.tensor_tensor(
+            out=cn_grouped[:],
+            in0=ct_ps[:].rearrange("p t s -> p s t"),
+            in1=gain[:].unsqueeze(1).to_broadcast([P, P, PACK]),
+            op=ALU.mult,
+        )
+        cn_codes = keep.tile([P, P], U32, align_bytes=64)
+        cn_scales = keep.tile([P, P], U8, align_bytes=64)
+        nc.vector.quantize_mx(
+            out=cn_codes[:].bitcast(FP8X4),
+            scales=cn_scales[:],
+            in_=cn_grouped[:].rearrange("p s t -> p (s t)"),
+        )
+
+        out_sb = keep.tile([P, HEADS, HEAD], F32)
+        out_rows = out.rearrange("b s h d -> (b s) h d")
+        for n in range(B_TILES):
+            if n % 2 == 0:
+                quantise_b(n + 1)
+            heads = slice(TILE_HEADS * n, TILE_HEADS * (n + 1))
+            q_ps = q_psum.tile([P, TILE_HEADS, HEAD], F32)
+            nc.tensor.matmul_mx(
+                out=q_ps[:].rearrange("p h d -> p (h d)"),
+                lhsT=cn_codes[:].bitcast(FP8X4),
+                lhsT_scale=cn_scales[:],
+                rhs=b_codes[:, n].bitcast(FP8X4),
+                rhs_scale=b_scales[:, n],
+                start=True,
+                stop=True,
+            )
+            sin = sin_cos[:, 0, heads, :]
+            cos = sin_cos[:, 1, heads, :]
+            rotated = out_sb[:, heads, NOPE:HEAD]
+            nc.vector.tensor_tensor(
+                out=rotated.rearrange("p h (f j) -> p h f j", f=2),
+                in0=q_ps[:, :, NOPE:HEAD].rearrange("p h (f j) -> p h f j", f=2),
+                in1=cos.unsqueeze(2).to_broadcast([P, TILE_HEADS, 2, HALF]),
+                op=ALU.mult,
+            )
+            cross = work.tile([P, TILE_HEADS, 2, HALF], F32)
+            nc.vector.scalar_tensor_tensor(
+                out=cross[:, :, 0, :], in0=q_ps[:, :, NOPE + HALF : HEAD], scalar=-1.0, in1=sin,
+                op0=ALU.mult, op1=ALU.mult,
+            )
+            nc.vector.tensor_tensor(
+                out=cross[:, :, 1, :], in0=q_ps[:, :, NOPE : NOPE + HALF], in1=sin, op=ALU.mult
+            )
+            nc.scalar.copy(out=out_sb[:, heads, 0:NOPE], in_=q_ps[:, :, 0:NOPE])
+            nc.gpsimd.tensor_tensor(
+                out=rotated, in0=rotated, in1=cross[:].rearrange("p h f j -> p h (f j)"), op=ALU.add
+            )
+            nc.sync.dma_start(out=out_rows[:, heads, :], in_=out_sb[:, heads, :])

@@ -30,7 +30,12 @@ A_PASSES = DIM // K_PASS
 B_TILES = HEADS * HEAD // N_TILE
 RUN = 4
 A_VECTOR_COLS = 320
-FIRST_PIECE = 128
+PART = TILE_HEADS * NOPE
+PLAIN = 0
+ROPE = 1
+GROUP_TILES = 2
+GROUPS = B_TILES // GROUP_TILES
+GROUP_HEADS = GROUP_TILES * TILE_HEADS
 
 FLOPS = 2 * P * DIM * QL + 2 * P * QL * HEADS * HEAD
 
@@ -48,7 +53,7 @@ def tile_mla_pa_s_kernel(tc, x, wq_a, q_norm_w, wq_b, out):
         keep = ctx.enter_context(tc.tile_pool(name="keep", bufs=1))
         work = ctx.enter_context(tc.tile_pool(name="work", bufs=2))
         psum = ctx.enter_context(tc.psum_pool(name="psum", bufs=1))
-        q_psum = ctx.enter_context(tc.psum_pool(name="q_psum", bufs=B_TILES))
+        q_psum = ctx.enter_context(tc.psum_pool(name="q_psum", bufs=GROUPS))
         ctx.enter_context(tc.manual_schedule())
 
         x_sb = keep.tile([P, DIM], BF16)
@@ -155,15 +160,36 @@ def tile_mla_pa_s_kernel(tc, x, wq_a, q_norm_w, wq_b, out):
                 stop=(g == A_PASSES - 1),
             )
 
-        b_grouped = keep.tile([P, B_TILES, PACK * N_TILE], BF16, align_bytes=64)
-        b_codes = keep.tile([P, B_TILES, N_TILE], U32, align_bytes=64)
-        b_scales = keep.tile([P, B_TILES, N_TILE], U8, align_bytes=64)
+        b_grouped = keep.tile([P, B_TILES, 2, PACK * PART], BF16, align_bytes=64)
+        b_codes = keep.tile([P, B_TILES, 2, PART], U32, align_bytes=64)
+        b_scales = keep.tile([P, B_TILES, 2, PART], U8, align_bytes=64)
 
-        def quantise_b(n):
-            nc.vector.quantize_mx(
-                out=b_codes[:, n].bitcast(FP8X4), scales=b_scales[:, n], in_=b_grouped[:, n]
+        def raw_part(n, part):
+            by_head = raw_b[n][:].rearrange("p t (h d) -> p t h d", d=HEAD)
+            return by_head[:, :, :, NOPE * part : NOPE * (part + 1)]
+
+        def regroup_plain(n):
+            nc.scalar.copy(
+                out=b_grouped[:, n, PLAIN].rearrange("p (h d t) -> p h d t", h=TILE_HEADS, t=PACK),
+                in_=raw_part(n, PLAIN).rearrange("p t h d -> p h d t"),
             )
 
+        def regroup_rope(n):
+            nc.vector.tensor_copy(
+                out=b_grouped[:, n, ROPE].rearrange(
+                    "p (h c i t) -> p h c t i", h=TILE_HEADS, i=RUN, t=PACK
+                ),
+                in_=raw_part(n, ROPE).rearrange("p t h (c i) -> p h c t i", i=RUN),
+            )
+
+        def quantise_b(n, part):
+            nc.vector.quantize_mx(
+                out=b_codes[:, n, part].bitcast(FP8X4),
+                scales=b_scales[:, n, part],
+                in_=b_grouped[:, n, part],
+            )
+
+        regroup_plain(0)
         squares = keep.tile([P, QL], F32)
         sum_squares = keep.tile([P, 1], F32)
         nc.scalar.activation(out=squares[:], in_=c_ps[:], func=ACT.Square, accum_out=sum_squares[:])
@@ -174,18 +200,24 @@ def tile_mla_pa_s_kernel(tc, x, wq_a, q_norm_w, wq_b, out):
         )
         inv_rms = keep.tile([P, 1], F32)
         nc.gpsimd.tensor_tensor(out=inv_rms[:], in0=mean_square[:], in1=minus_half[:], op=ALU.pow)
-        regroup(nc.vector.tensor_copy, b_grouped[:, 0], raw_b[0], 0, N_TILE)
-        quantise_b(0)
-        regroup(nc.scalar.copy, b_grouped[:, 1], raw_b[1], 0, FIRST_PIECE)
+        regroup_rope(0)
+        regroup_rope(1)
+        quantise_b(0, ROPE)
+        quantise_b(0, PLAIN)
+        quantise_b(1, ROPE)
+        regroup_plain(1)
         c_scaled = keep.tile([P, QL], F32)
         nc.scalar.activation(out=c_scaled[:], in_=c_ps[:], func=ACT.Copy, scale=inv_rms[:, 0:1])
         ct_ps = psum.tile([P, PACK, P], F32)
         for t in range(PACK):
             nc.tensor.transpose(ct_ps[:, t, :], c_scaled[:, P * t : P * (t + 1)], ident[:])
-        regroup(nc.scalar.copy, b_grouped[:, 1], raw_b[1], FIRST_PIECE, N_TILE)
-        regroup(nc.vector.tensor_copy, b_grouped[:, 2], raw_b[2], 0, N_TILE)
-        quantise_b(2)
-        regroup(nc.scalar.copy, b_grouped[:, 3], raw_b[3], 0, N_TILE)
+        regroup_rope(2)
+        regroup_rope(3)
+        quantise_b(2, ROPE)
+        quantise_b(3, ROPE)
+        quantise_b(1, PLAIN)
+        regroup_plain(2)
+        regroup_plain(3)
         cn_grouped = keep.tile([P, P, PACK], BF16, align_bytes=64)
         nc.vector.tensor_tensor(
             out=cn_grouped[:],
@@ -203,39 +235,80 @@ def tile_mla_pa_s_kernel(tc, x, wq_a, q_norm_w, wq_b, out):
 
         out_sb = keep.tile([P, HEADS, HEAD], F32)
         out_rows = out.rearrange("b s h d -> (b s) h d")
-        for n in range(B_TILES):
-            if n % 2 == 0:
-                quantise_b(n + 1)
-            heads = slice(TILE_HEADS * n, TILE_HEADS * (n + 1))
-            q_ps = q_psum.tile([P, TILE_HEADS, HEAD], F32)
-            nc.tensor.matmul_mx(
-                out=q_ps[:].rearrange("p h d -> p (h d)"),
-                lhsT=cn_codes[:].bitcast(FP8X4),
-                lhsT_scale=cn_scales[:],
-                rhs=b_codes[:, n].bitcast(FP8X4),
-                rhs_scale=b_scales[:, n],
-                start=True,
-                stop=True,
-            )
+
+        def project(bank, group, part):
+            for i in range(GROUP_TILES):
+                n = GROUP_TILES * group + i
+                nc.tensor.matmul_mx(
+                    out=bank[:, TILE_HEADS * i : TILE_HEADS * (i + 1), :].rearrange(
+                        "p h d -> p (h d)"
+                    ),
+                    lhsT=cn_codes[:].bitcast(FP8X4),
+                    lhsT_scale=cn_scales[:],
+                    rhs=b_codes[:, n, part].bitcast(FP8X4),
+                    rhs_scale=b_scales[:, n, part],
+                    start=True,
+                    stop=True,
+                )
+
+        def products(rope_ps, cross, group):
+            heads = slice(GROUP_HEADS * group, GROUP_HEADS * (group + 1))
             sin = sin_cos[:, 0, heads, :]
             cos = sin_cos[:, 1, heads, :]
-            rotated = out_sb[:, heads, NOPE:HEAD]
             nc.vector.tensor_tensor(
-                out=rotated.rearrange("p h (f j) -> p h f j", f=2),
-                in0=q_ps[:, :, NOPE:HEAD].rearrange("p h (f j) -> p h f j", f=2),
-                in1=cos.unsqueeze(2).to_broadcast([P, TILE_HEADS, 2, HALF]),
+                out=out_sb[:, heads, NOPE:HEAD].rearrange("p h (f j) -> p h f j", f=2),
+                in0=rope_ps[:].rearrange("p h (f j) -> p h f j", f=2),
+                in1=cos.unsqueeze(2).to_broadcast([P, GROUP_HEADS, 2, HALF]),
                 op=ALU.mult,
             )
-            cross = work.tile([P, TILE_HEADS, 2, HALF], F32)
             nc.vector.scalar_tensor_tensor(
-                out=cross[:, :, 0, :], in0=q_ps[:, :, NOPE + HALF : HEAD], scalar=-1.0, in1=sin,
+                out=cross[:, :, 0, :], in0=rope_ps[:, :, HALF:NOPE], scalar=-1.0, in1=sin,
                 op0=ALU.mult, op1=ALU.mult,
             )
             nc.vector.tensor_tensor(
-                out=cross[:, :, 1, :], in0=q_ps[:, :, NOPE : NOPE + HALF], in1=sin, op=ALU.mult
+                out=cross[:, :, 1, :], in0=rope_ps[:, :, 0:HALF], in1=sin, op=ALU.mult
             )
-            nc.scalar.copy(out=out_sb[:, heads, 0:NOPE], in_=q_ps[:, :, 0:NOPE])
-            nc.gpsimd.tensor_tensor(
-                out=rotated, in0=rotated, in1=cross[:].rearrange("p h f j -> p h (f j)"), op=ALU.add
-            )
-            nc.sync.dma_start(out=out_rows[:, heads, :], in_=out_sb[:, heads, :])
+
+        def copy_plain(plain_ps, group):
+            heads = slice(GROUP_HEADS * group, GROUP_HEADS * (group + 1))
+            nc.scalar.copy(out=out_sb[:, heads, 0:NOPE], in_=plain_ps[:])
+
+        def add_and_store(engine, cross, group):
+            for i in range(GROUP_TILES):
+                first = GROUP_HEADS * group + TILE_HEADS * i
+                heads = slice(first, first + TILE_HEADS)
+                rotated = out_sb[:, heads, NOPE:HEAD]
+                engine.tensor_tensor(
+                    out=rotated,
+                    in0=rotated,
+                    in1=cross[:, TILE_HEADS * i : TILE_HEADS * (i + 1)].rearrange(
+                        "p h f j -> p h (f j)"
+                    ),
+                    op=ALU.add,
+                )
+                nc.sync.dma_start(out=out_rows[:, heads, :], in_=out_sb[:, heads, :])
+
+        rope_banks = [
+            q_psum.tile([P, GROUP_HEADS, NOPE], F32, name="rope_ps%d" % g, tag="rope_ps")
+            for g in range(GROUPS)
+        ]
+        plain_banks = [
+            q_psum.tile([P, GROUP_HEADS, NOPE], F32, name="plain_ps%d" % g, tag="plain_ps")
+            for g in range(GROUPS)
+        ]
+        crosses = [
+            work.tile([P, GROUP_HEADS, 2, HALF], F32, name="cross%d" % g, tag="cross")
+            for g in range(GROUPS)
+        ]
+        project(rope_banks[0], 0, ROPE)
+        project(plain_banks[0], 0, PLAIN)
+        project(rope_banks[1], 1, ROPE)
+        products(rope_banks[0], crosses[0], 0)
+        products(rope_banks[1], crosses[1], 1)
+        copy_plain(plain_banks[0], 0)
+        add_and_store(nc.gpsimd, crosses[0], 0)
+        quantise_b(2, PLAIN)
+        quantise_b(3, PLAIN)
+        project(plain_banks[1], 1, PLAIN)
+        copy_plain(plain_banks[1], 1)
+        add_and_store(nc.vector, crosses[1], 1)

@@ -30,12 +30,7 @@ A_PASSES = DIM // K_PASS
 B_TILES = HEADS * HEAD // N_TILE
 RUN = 4
 A_VECTOR_COLS = 320
-PART = TILE_HEADS * NOPE
-PLAIN = 0
-ROPE = 1
-GROUP_TILES = 2
-GROUPS = B_TILES // GROUP_TILES
-GROUP_HEADS = GROUP_TILES * TILE_HEADS
+FIRST_PIECE = 128
 
 FLOPS = 2 * P * DIM * QL + 2 * P * QL * HEADS * HEAD
 
@@ -53,7 +48,7 @@ def tile_mla_pa_s_kernel(tc, x, wq_a, q_norm_w, wq_b, out):
         keep = ctx.enter_context(tc.tile_pool(name="keep", bufs=1))
         work = ctx.enter_context(tc.tile_pool(name="work", bufs=2))
         psum = ctx.enter_context(tc.psum_pool(name="psum", bufs=1))
-        q_psum = ctx.enter_context(tc.psum_pool(name="q_psum", bufs=GROUPS))
+        q_psum = ctx.enter_context(tc.psum_pool(name="q_psum", bufs=B_TILES))
         ctx.enter_context(tc.manual_schedule())
 
         x_sb = keep.tile([P, DIM], BF16)
@@ -106,19 +101,16 @@ def tile_mla_pa_s_kernel(tc, x, wq_a, q_norm_w, wq_b, out):
             out=position[:], in0=position_i[:], scalar1=FIRST_POSITION, scalar2=1.0 / (2.0 * math.pi),
             op0=ALU.add, op1=ALU.mult,
         )
-        turns = keep.tile([P, 2, HEADS, HALF], F32)
+        turns = keep.tile([P, HEADS, HALF], F32)
         nc.vector.tensor_tensor(
-            out=turns[:, 0],
+            out=turns[:],
             in0=position[:].unsqueeze(2).to_broadcast([P, HEADS, HALF]),
             in1=theta[:].unsqueeze(1).to_broadcast([P, HEADS, HALF]),
             op=ALU.mult,
         )
-        nc.vector.tensor_scalar_add(out=turns[:, 1], in0=turns[:, 0], scalar1=0.25)
-        whole = keep.tile([P, 2, HEADS, HALF], I32)
+        whole = keep.tile([P, HEADS, HALF], I32)
         nc.vector.tensor_copy(out=whole[:], in_=turns[:])
         nc.vector.tensor_tensor(out=turns[:], in0=turns[:], in1=whole[:], op=ALU.subtract)
-        sin_cos = keep.tile([P, 2, HEADS, HALF], F32)
-        nc.scalar.activation(out=sin_cos[:], in_=turns[:], func=ACT.Sin, scale=2.0 * math.pi)
 
         x_words = x_sb[:].bitcast(F32)
         xt_ps = psum.tile([P, 2 * A_PASSES, P], F32)
@@ -137,7 +129,8 @@ def tile_mla_pa_s_kernel(tc, x, wq_a, q_norm_w, wq_b, out):
                 out=a_codes[:, g].bitcast(FP8X4), scales=a_scales[:, g], in_=a_grouped[:, g]
             )
 
-        regroup(nc.vector.tensor_copy, a_grouped[:, 0], raw_a[0], 0, QL)
+        regroup(nc.vector.tensor_copy, a_grouped[:, 0], raw_a[0], 0, A_VECTOR_COLS)
+        regroup(nc.scalar.copy, a_grouped[:, 0], raw_a[0], A_VECTOR_COLS, QL)
         quantise_a(0)
         nc.scalar.copy(
             out=x_grouped[:].bitcast(F32).rearrange("q (g s u) -> q g s u", g=A_PASSES, u=2),
@@ -147,6 +140,12 @@ def tile_mla_pa_s_kernel(tc, x, wq_a, q_norm_w, wq_b, out):
         regroup(nc.scalar.copy, a_grouped[:, 1], raw_a[1], A_VECTOR_COLS, QL)
         nc.vector.quantize_mx(out=x_codes[:].bitcast(FP8X4), scales=x_scales[:], in_=x_grouped[:])
         quantise_a(1)
+
+        sin_cos = keep.tile([P, 2, HEADS, HALF], F32)
+        half_sin = keep.tile([P, HEADS, HALF], F32)
+        nc.scalar.activation(out=sin_cos[:, 0], in_=turns[:], func=ACT.Sin, scale=2.0 * math.pi)
+        nc.scalar.activation(out=half_sin[:], in_=turns[:], func=ACT.Sin, scale=math.pi)
+        nc.scalar.activation(out=half_sin[:], in_=half_sin[:], func=ACT.Square)
 
         c_ps = psum.tile([P, QL], F32)
         for g in range(A_PASSES):
@@ -160,36 +159,15 @@ def tile_mla_pa_s_kernel(tc, x, wq_a, q_norm_w, wq_b, out):
                 stop=(g == A_PASSES - 1),
             )
 
-        b_grouped = keep.tile([P, B_TILES, 2, PACK * PART], BF16, align_bytes=64)
-        b_codes = keep.tile([P, B_TILES, 2, PART], U32, align_bytes=64)
-        b_scales = keep.tile([P, B_TILES, 2, PART], U8, align_bytes=64)
+        b_grouped = keep.tile([P, B_TILES, PACK * N_TILE], BF16, align_bytes=64)
+        b_codes = keep.tile([P, B_TILES, N_TILE], U32, align_bytes=64)
+        b_scales = keep.tile([P, B_TILES, N_TILE], U8, align_bytes=64)
 
-        def raw_part(n, part):
-            by_head = raw_b[n][:].rearrange("p t (h d) -> p t h d", d=HEAD)
-            return by_head[:, :, :, NOPE * part : NOPE * (part + 1)]
-
-        def regroup_plain(n):
-            nc.scalar.copy(
-                out=b_grouped[:, n, PLAIN].rearrange("p (h d t) -> p h d t", h=TILE_HEADS, t=PACK),
-                in_=raw_part(n, PLAIN).rearrange("p t h d -> p h d t"),
-            )
-
-        def regroup_rope(n):
-            nc.vector.tensor_copy(
-                out=b_grouped[:, n, ROPE].rearrange(
-                    "p (h c i t) -> p h c t i", h=TILE_HEADS, i=RUN, t=PACK
-                ),
-                in_=raw_part(n, ROPE).rearrange("p t h (c i) -> p h c t i", i=RUN),
-            )
-
-        def quantise_b(n, part):
+        def quantise_b(n):
             nc.vector.quantize_mx(
-                out=b_codes[:, n, part].bitcast(FP8X4),
-                scales=b_scales[:, n, part],
-                in_=b_grouped[:, n, part],
+                out=b_codes[:, n].bitcast(FP8X4), scales=b_scales[:, n], in_=b_grouped[:, n]
             )
 
-        regroup_plain(0)
         squares = keep.tile([P, QL], F32)
         sum_squares = keep.tile([P, 1], F32)
         nc.scalar.activation(out=squares[:], in_=c_ps[:], func=ACT.Square, accum_out=sum_squares[:])
@@ -200,24 +178,21 @@ def tile_mla_pa_s_kernel(tc, x, wq_a, q_norm_w, wq_b, out):
         )
         inv_rms = keep.tile([P, 1], F32)
         nc.gpsimd.tensor_tensor(out=inv_rms[:], in0=mean_square[:], in1=minus_half[:], op=ALU.pow)
-        regroup_rope(0)
-        regroup_rope(1)
-        quantise_b(0, ROPE)
-        quantise_b(0, PLAIN)
-        quantise_b(1, ROPE)
-        regroup_plain(1)
+        nc.gpsimd.tensor_scalar(
+            out=sin_cos[:, 1], in0=half_sin[:], scalar1=-2.0, scalar2=1.0, op0=ALU.mult, op1=ALU.add
+        )
+        regroup(nc.vector.tensor_copy, b_grouped[:, 0], raw_b[0], 0, N_TILE)
+        regroup(nc.vector.tensor_copy, b_grouped[:, 1], raw_b[1], 0, N_TILE)
+        quantise_b(0)
+        quantise_b(1)
+        regroup(nc.scalar.copy, b_grouped[:, 2], raw_b[2], 0, FIRST_PIECE)
         c_scaled = keep.tile([P, QL], F32)
         nc.scalar.activation(out=c_scaled[:], in_=c_ps[:], func=ACT.Copy, scale=inv_rms[:, 0:1])
         ct_ps = psum.tile([P, PACK, P], F32)
         for t in range(PACK):
             nc.tensor.transpose(ct_ps[:, t, :], c_scaled[:, P * t : P * (t + 1)], ident[:])
-        regroup_rope(2)
-        regroup_rope(3)
-        quantise_b(2, ROPE)
-        quantise_b(3, ROPE)
-        quantise_b(1, PLAIN)
-        regroup_plain(2)
-        regroup_plain(3)
+        regroup(nc.scalar.copy, b_grouped[:, 2], raw_b[2], FIRST_PIECE, N_TILE)
+        regroup(nc.scalar.copy, b_grouped[:, 3], raw_b[3], 0, N_TILE)
         cn_grouped = keep.tile([P, P, PACK], BF16, align_bytes=64)
         nc.vector.tensor_tensor(
             out=cn_grouped[:],
@@ -235,80 +210,40 @@ def tile_mla_pa_s_kernel(tc, x, wq_a, q_norm_w, wq_b, out):
 
         out_sb = keep.tile([P, HEADS, HEAD], F32)
         out_rows = out.rearrange("b s h d -> (b s) h d")
-
-        def project(bank, group, part):
-            for i in range(GROUP_TILES):
-                n = GROUP_TILES * group + i
-                nc.tensor.matmul_mx(
-                    out=bank[:, TILE_HEADS * i : TILE_HEADS * (i + 1), :].rearrange(
-                        "p h d -> p (h d)"
-                    ),
-                    lhsT=cn_codes[:].bitcast(FP8X4),
-                    lhsT_scale=cn_scales[:],
-                    rhs=b_codes[:, n, part].bitcast(FP8X4),
-                    rhs_scale=b_scales[:, n, part],
-                    start=True,
-                    stop=True,
-                )
-
-        def products(rope_ps, cross, group):
-            heads = slice(GROUP_HEADS * group, GROUP_HEADS * (group + 1))
+        for n in range(B_TILES):
+            if n % 2 == 0:
+                quantise_b(n // 2 + 2)
+            heads = slice(TILE_HEADS * n, TILE_HEADS * (n + 1))
+            q_ps = q_psum.tile([P, TILE_HEADS, HEAD], F32)
+            nc.tensor.matmul_mx(
+                out=q_ps[:].rearrange("p h d -> p (h d)"),
+                lhsT=cn_codes[:].bitcast(FP8X4),
+                lhsT_scale=cn_scales[:],
+                rhs=b_codes[:, n].bitcast(FP8X4),
+                rhs_scale=b_scales[:, n],
+                start=True,
+                stop=True,
+            )
             sin = sin_cos[:, 0, heads, :]
             cos = sin_cos[:, 1, heads, :]
+            rotated = out_sb[:, heads, NOPE:HEAD]
             nc.vector.tensor_tensor(
-                out=out_sb[:, heads, NOPE:HEAD].rearrange("p h (f j) -> p h f j", f=2),
-                in0=rope_ps[:].rearrange("p h (f j) -> p h f j", f=2),
-                in1=cos.unsqueeze(2).to_broadcast([P, GROUP_HEADS, 2, HALF]),
+                out=rotated.rearrange("p h (f j) -> p h f j", f=2),
+                in0=q_ps[:, :, NOPE:HEAD].rearrange("p h (f j) -> p h f j", f=2),
+                in1=cos.unsqueeze(2).to_broadcast([P, TILE_HEADS, 2, HALF]),
                 op=ALU.mult,
             )
+            cross = work.tile([P, TILE_HEADS, 2, HALF], F32)
             nc.vector.scalar_tensor_tensor(
-                out=cross[:, :, 0, :], in0=rope_ps[:, :, HALF:NOPE], scalar=-1.0, in1=sin,
+                out=cross[:, :, 0, :], in0=q_ps[:, :, NOPE + HALF : HEAD], scalar=-1.0, in1=sin,
                 op0=ALU.mult, op1=ALU.mult,
             )
             nc.vector.tensor_tensor(
-                out=cross[:, :, 1, :], in0=rope_ps[:, :, 0:HALF], in1=sin, op=ALU.mult
+                out=cross[:, :, 1, :], in0=q_ps[:, :, NOPE : NOPE + HALF], in1=sin, op=ALU.mult
             )
-
-        def copy_plain(plain_ps, group):
-            heads = slice(GROUP_HEADS * group, GROUP_HEADS * (group + 1))
-            nc.scalar.copy(out=out_sb[:, heads, 0:NOPE], in_=plain_ps[:])
-
-        def add_and_store(engine, cross, group):
-            for i in range(GROUP_TILES):
-                first = GROUP_HEADS * group + TILE_HEADS * i
-                heads = slice(first, first + TILE_HEADS)
-                rotated = out_sb[:, heads, NOPE:HEAD]
-                engine.tensor_tensor(
-                    out=rotated,
-                    in0=rotated,
-                    in1=cross[:, TILE_HEADS * i : TILE_HEADS * (i + 1)].rearrange(
-                        "p h f j -> p h (f j)"
-                    ),
-                    op=ALU.add,
-                )
-                nc.sync.dma_start(out=out_rows[:, heads, :], in_=out_sb[:, heads, :])
-
-        rope_banks = [
-            q_psum.tile([P, GROUP_HEADS, NOPE], F32, name="rope_ps%d" % g, tag="rope_ps")
-            for g in range(GROUPS)
-        ]
-        plain_banks = [
-            q_psum.tile([P, GROUP_HEADS, NOPE], F32, name="plain_ps%d" % g, tag="plain_ps")
-            for g in range(GROUPS)
-        ]
-        crosses = [
-            work.tile([P, GROUP_HEADS, 2, HALF], F32, name="cross%d" % g, tag="cross")
-            for g in range(GROUPS)
-        ]
-        project(rope_banks[0], 0, ROPE)
-        project(plain_banks[0], 0, PLAIN)
-        project(rope_banks[1], 1, ROPE)
-        products(rope_banks[0], crosses[0], 0)
-        products(rope_banks[1], crosses[1], 1)
-        copy_plain(plain_banks[0], 0)
-        add_and_store(nc.gpsimd, crosses[0], 0)
-        quantise_b(2, PLAIN)
-        quantise_b(3, PLAIN)
-        project(plain_banks[1], 1, PLAIN)
-        copy_plain(plain_banks[1], 1)
-        add_and_store(nc.vector, crosses[1], 1)
+            nc.scalar.copy(out=out_sb[:, heads, 0:NOPE], in_=q_ps[:, :, 0:NOPE])
+            adder = nc.gpsimd if n + 1 < B_TILES else nc.vector
+            adder.tensor_tensor(
+                out=rotated, in0=rotated, in1=cross[:].rearrange("p h f j -> p h (f j)"), op=ALU.add
+            )
+            nc.sync.dma_start(out=out_rows[:, heads, :], in_=out_sb[:, heads, :])

@@ -24,13 +24,16 @@ NOPE = 64
 HALF = 32
 FIRST_POSITION = 37
 EPS = 1e-6
+THETA_1 = 10000.0 ** (-1.0 / HALF)
+WRAPPED = 16
+assert (P - 1 + FIRST_POSITION) * THETA_1**WRAPPED < math.pi
 N_TILE = 512
 TILE_HEADS = N_TILE // HEAD
 A_PASSES = DIM // K_PASS
 B_TILES = HEADS * HEAD // N_TILE
 RUN = 4
 A_VECTOR_COLS = 320
-FIRST_PIECE = 128
+FIRST_PIECE = 320
 
 FLOPS = 2 * P * DIM * QL + 2 * P * QL * HEADS * HEAD
 
@@ -84,33 +87,28 @@ def tile_mla_pa_s_kernel(tc, x, wq_a, q_norm_w, wq_b, out):
         warm = keep.tile([P, 1], F32)
         nc.scalar.activation(out=warm[:], in_=minus_half[:], func=ACT.Sin)
 
-        theta_1 = 10000.0 ** (-1.0 / HALF)
-        theta = keep.tile([P, HALF], F32)
-        nc.vector.memset(theta[:, 0:1], 1.0)
-        w = 1
-        while w < HALF:
-            nc.vector.tensor_scalar_mul(
-                out=theta[:, w : 2 * w], in0=theta[:, 0:w], scalar1=theta_1**w
-            )
-            w *= 2
+        turns = keep.tile([P, HEADS, HALF], F32)
         nc.vector.tensor_single_scalar(
             out=position_i[:], in_=position_i[:], scalar=P - 1, op=ALU.bitwise_and
         )
-        position = keep.tile([P, HEADS], F32)
         nc.vector.tensor_scalar(
-            out=position[:], in0=position_i[:], scalar1=FIRST_POSITION, scalar2=1.0 / (2.0 * math.pi),
+            out=turns[:, :, 0], in0=position_i[:], scalar1=FIRST_POSITION, scalar2=1.0 / (2.0 * math.pi),
             op0=ALU.add, op1=ALU.mult,
         )
-        turns = keep.tile([P, HEADS, HALF], F32)
+        w = 1
+        while w < HALF:
+            nc.vector.tensor_scalar_mul(
+                out=turns[:, :, w : 2 * w], in0=turns[:, :, 0:w], scalar1=THETA_1**w
+            )
+            w *= 2
+        whole = keep.tile([P, HEADS, WRAPPED], I32)
+        nc.vector.tensor_copy(out=whole[:], in_=turns[:, :, 0:WRAPPED])
         nc.vector.tensor_tensor(
-            out=turns[:],
-            in0=position[:].unsqueeze(2).to_broadcast([P, HEADS, HALF]),
-            in1=theta[:].unsqueeze(1).to_broadcast([P, HEADS, HALF]),
-            op=ALU.mult,
+            out=turns[:, :, 0:WRAPPED], in0=turns[:, :, 0:WRAPPED], in1=whole[:], op=ALU.subtract
         )
-        whole = keep.tile([P, HEADS, HALF], I32)
-        nc.vector.tensor_copy(out=whole[:], in_=turns[:])
-        nc.vector.tensor_tensor(out=turns[:], in0=turns[:], in1=whole[:], op=ALU.subtract)
+        sin_cos = keep.tile([P, 2, HEADS, HALF], F32)
+        half_sin = keep.tile([P, HEADS, HALF], F32)
+        nc.scalar.activation(out=sin_cos[:, 0], in_=turns[:], func=ACT.Sin, scale=2.0 * math.pi)
 
         x_words = x_sb[:].bitcast(F32)
         xt_ps = psum.tile([P, 2 * A_PASSES, P], F32)
@@ -141,12 +139,6 @@ def tile_mla_pa_s_kernel(tc, x, wq_a, q_norm_w, wq_b, out):
         nc.vector.quantize_mx(out=x_codes[:].bitcast(FP8X4), scales=x_scales[:], in_=x_grouped[:])
         quantise_a(1)
 
-        sin_cos = keep.tile([P, 2, HEADS, HALF], F32)
-        half_sin = keep.tile([P, HEADS, HALF], F32)
-        nc.scalar.activation(out=sin_cos[:, 0], in_=turns[:], func=ACT.Sin, scale=2.0 * math.pi)
-        nc.scalar.activation(out=half_sin[:], in_=turns[:], func=ACT.Sin, scale=math.pi)
-        nc.scalar.activation(out=half_sin[:], in_=half_sin[:], func=ACT.Square)
-
         c_ps = psum.tile([P, QL], F32)
         for g in range(A_PASSES):
             nc.tensor.matmul_mx(
@@ -168,31 +160,36 @@ def tile_mla_pa_s_kernel(tc, x, wq_a, q_norm_w, wq_b, out):
                 out=b_codes[:, n].bitcast(FP8X4), scales=b_scales[:, n], in_=b_grouped[:, n]
             )
 
+        regroup(nc.scalar.copy, b_grouped[:, 0], raw_b[0], 0, FIRST_PIECE)
         squares = keep.tile([P, QL], F32)
         sum_squares = keep.tile([P, 1], F32)
         nc.scalar.activation(out=squares[:], in_=c_ps[:], func=ACT.Square, accum_out=sum_squares[:])
         mean_square = keep.tile([P, 1], F32)
-        nc.gpsimd.tensor_scalar(
-            out=mean_square[:], in0=sum_squares[:], scalar1=1.0 / QL, scalar2=EPS,
-            op0=ALU.mult, op1=ALU.add,
+        nc.scalar.activation(
+            out=mean_square[:], in_=sum_squares[:], func=ACT.Copy, scale=1.0 / QL, bias=EPS
         )
         inv_rms = keep.tile([P, 1], F32)
         nc.gpsimd.tensor_tensor(out=inv_rms[:], in0=mean_square[:], in1=minus_half[:], op=ALU.pow)
+        regroup(nc.scalar.copy, b_grouped[:, 0], raw_b[0], FIRST_PIECE, N_TILE)
+        for n in range(1, B_TILES - 1):
+            regroup(nc.vector.tensor_copy, b_grouped[:, n], raw_b[n], 0, N_TILE)
+        for n in range(B_TILES - 1):
+            quantise_b(n)
+        c_scaled = keep.tile([P, QL], F32)
+        ct_ps = psum.tile([P, PACK, P], F32)
+        for half in range(2):
+            cols = slice(QL // 2 * half, QL // 2 * (half + 1))
+            nc.scalar.activation(
+                out=c_scaled[:, cols], in_=c_ps[:, cols], func=ACT.Copy, scale=inv_rms[:, 0:1]
+            )
+            for t in range(PACK // 2 * half, PACK // 2 * (half + 1)):
+                nc.tensor.transpose(ct_ps[:, t, :], c_scaled[:, P * t : P * (t + 1)], ident[:])
+        nc.scalar.activation(out=half_sin[:], in_=turns[:], func=ACT.Sin, scale=math.pi)
+        nc.scalar.activation(out=half_sin[:], in_=half_sin[:], func=ACT.Square)
         nc.gpsimd.tensor_scalar(
             out=sin_cos[:, 1], in0=half_sin[:], scalar1=-2.0, scalar2=1.0, op0=ALU.mult, op1=ALU.add
         )
-        regroup(nc.vector.tensor_copy, b_grouped[:, 0], raw_b[0], 0, N_TILE)
-        regroup(nc.vector.tensor_copy, b_grouped[:, 1], raw_b[1], 0, N_TILE)
-        quantise_b(0)
-        quantise_b(1)
-        regroup(nc.scalar.copy, b_grouped[:, 2], raw_b[2], 0, FIRST_PIECE)
-        c_scaled = keep.tile([P, QL], F32)
-        nc.scalar.activation(out=c_scaled[:], in_=c_ps[:], func=ACT.Copy, scale=inv_rms[:, 0:1])
-        ct_ps = psum.tile([P, PACK, P], F32)
-        for t in range(PACK):
-            nc.tensor.transpose(ct_ps[:, t, :], c_scaled[:, P * t : P * (t + 1)], ident[:])
-        regroup(nc.scalar.copy, b_grouped[:, 2], raw_b[2], FIRST_PIECE, N_TILE)
-        regroup(nc.scalar.copy, b_grouped[:, 3], raw_b[3], 0, N_TILE)
+        regroup(nc.scalar.copy, b_grouped[:, B_TILES - 1], raw_b[B_TILES - 1], 0, N_TILE)
         cn_grouped = keep.tile([P, P, PACK], BF16, align_bytes=64)
         nc.vector.tensor_tensor(
             out=cn_grouped[:],
@@ -211,8 +208,8 @@ def tile_mla_pa_s_kernel(tc, x, wq_a, q_norm_w, wq_b, out):
         out_sb = keep.tile([P, HEADS, HEAD], F32)
         out_rows = out.rearrange("b s h d -> (b s) h d")
         for n in range(B_TILES):
-            if n % 2 == 0:
-                quantise_b(n // 2 + 2)
+            if n == B_TILES - 2:
+                quantise_b(B_TILES - 1)
             heads = slice(TILE_HEADS * n, TILE_HEADS * (n + 1))
             q_ps = q_psum.tile([P, TILE_HEADS, HEAD], F32)
             nc.tensor.matmul_mx(

@@ -33,7 +33,7 @@ A_PASSES = DIM // K_PASS
 B_TILES = HEADS * HEAD // N_TILE
 RUN = 4
 A_VECTOR_COLS = 320
-FIRST_PIECE = 320
+B_VECTOR_COLS = 1280
 
 FLOPS = 2 * P * DIM * QL + 2 * P * QL * HEADS * HEAD
 
@@ -68,15 +68,15 @@ def tile_mla_pa_s_kernel(tc, x, wq_a, q_norm_w, wq_b, out):
         load_a(0)
         nc.sync.dma_start(out=x_sb[:], in_=x.rearrange("b s k -> (b s) k"))
         load_a(1)
+        gain = keep.tile([P, PACK], BF16)
+        with nc.allow_non_contiguous_dma(reason="512 single values"):
+            nc.sync.dma_start(out=gain[:], in_=q_norm_w.rearrange("(t p) -> p t", p=P))
         raw_b = [keep.tile([P, PACK, N_TILE], BF16, name="raw_b%d" % n) for n in range(B_TILES)]
         for n in range(B_TILES):
             nc.sync.dma_start(
                 out=raw_b[n][:],
                 in_=wq_b[:, N_TILE * n : N_TILE * (n + 1)].rearrange("(t p) c -> p t c", p=P),
             )
-        gain = keep.tile([P, PACK], BF16)
-        with nc.allow_non_contiguous_dma(reason="512 gains, one to a partition and value"):
-            nc.scalar.dma_start(out=gain[:], in_=q_norm_w.rearrange("(t p) -> p t", p=P))
 
         position_i = keep.tile([P, HEADS], I32)
         nc.gpsimd.iota(position_i[:], pattern=[[1, HEADS]], base=0, channel_multiplier=HEADS)
@@ -139,6 +139,8 @@ def tile_mla_pa_s_kernel(tc, x, wq_a, q_norm_w, wq_b, out):
         nc.vector.quantize_mx(out=x_codes[:].bitcast(FP8X4), scales=x_scales[:], in_=x_grouped[:])
         quantise_a(1)
 
+        nc.scalar.activation(out=half_sin[:], in_=turns[:], func=ACT.Sin, scale=math.pi)
+
         c_ps = psum.tile([P, QL], F32)
         for g in range(A_PASSES):
             nc.tensor.matmul_mx(
@@ -155,12 +157,14 @@ def tile_mla_pa_s_kernel(tc, x, wq_a, q_norm_w, wq_b, out):
         b_codes = keep.tile([P, B_TILES, N_TILE], U32, align_bytes=64)
         b_scales = keep.tile([P, B_TILES, N_TILE], U8, align_bytes=64)
 
+        def vector_cols(n):
+            return min(max(B_VECTOR_COLS - N_TILE * n, 0), N_TILE)
+
         def quantise_b(n):
             nc.vector.quantize_mx(
                 out=b_codes[:, n].bitcast(FP8X4), scales=b_scales[:, n], in_=b_grouped[:, n]
             )
 
-        regroup(nc.scalar.copy, b_grouped[:, 0], raw_b[0], 0, FIRST_PIECE)
         squares = keep.tile([P, QL], F32)
         sum_squares = keep.tile([P, 1], F32)
         nc.scalar.activation(out=squares[:], in_=c_ps[:], func=ACT.Square, accum_out=sum_squares[:])
@@ -170,11 +174,13 @@ def tile_mla_pa_s_kernel(tc, x, wq_a, q_norm_w, wq_b, out):
         )
         inv_rms = keep.tile([P, 1], F32)
         nc.gpsimd.tensor_tensor(out=inv_rms[:], in0=mean_square[:], in1=minus_half[:], op=ALU.pow)
-        regroup(nc.scalar.copy, b_grouped[:, 0], raw_b[0], FIRST_PIECE, N_TILE)
-        for n in range(1, B_TILES - 1):
-            regroup(nc.vector.tensor_copy, b_grouped[:, n], raw_b[n], 0, N_TILE)
-        for n in range(B_TILES - 1):
-            quantise_b(n)
+        nc.scalar.activation(out=half_sin[:], in_=half_sin[:], func=ACT.Square)
+        own = [n for n in range(B_TILES) if vector_cols(n) == N_TILE]
+        for n in range(B_TILES):
+            if vector_cols(n) > 0:
+                regroup(nc.vector.tensor_copy, b_grouped[:, n], raw_b[n], 0, vector_cols(n))
+            if n - 1 in own:
+                quantise_b(n - 1)
         c_scaled = keep.tile([P, QL], F32)
         ct_ps = psum.tile([P, PACK, P], F32)
         for half in range(2):
@@ -184,12 +190,12 @@ def tile_mla_pa_s_kernel(tc, x, wq_a, q_norm_w, wq_b, out):
             )
             for t in range(PACK // 2 * half, PACK // 2 * (half + 1)):
                 nc.tensor.transpose(ct_ps[:, t, :], c_scaled[:, P * t : P * (t + 1)], ident[:])
-        nc.scalar.activation(out=half_sin[:], in_=turns[:], func=ACT.Sin, scale=math.pi)
-        nc.scalar.activation(out=half_sin[:], in_=half_sin[:], func=ACT.Square)
         nc.gpsimd.tensor_scalar(
             out=sin_cos[:, 1], in0=half_sin[:], scalar1=-2.0, scalar2=1.0, op0=ALU.mult, op1=ALU.add
         )
-        regroup(nc.scalar.copy, b_grouped[:, B_TILES - 1], raw_b[B_TILES - 1], 0, N_TILE)
+        for n in range(B_TILES):
+            if vector_cols(n) < N_TILE:
+                regroup(nc.scalar.copy, b_grouped[:, n], raw_b[n], vector_cols(n), N_TILE)
         cn_grouped = keep.tile([P, P, PACK], BF16, align_bytes=64)
         nc.vector.tensor_tensor(
             out=cn_grouped[:],
@@ -207,9 +213,10 @@ def tile_mla_pa_s_kernel(tc, x, wq_a, q_norm_w, wq_b, out):
 
         out_sb = keep.tile([P, HEADS, HEAD], F32)
         out_rows = out.rearrange("b s h d -> (b s) h d")
+        late = [n for n in range(B_TILES) if n not in own]
         for n in range(B_TILES):
-            if n == B_TILES - 2:
-                quantise_b(B_TILES - 1)
+            if n % 2 == 0 and n // 2 < len(late):
+                quantise_b(late[n // 2])
             heads = slice(TILE_HEADS * n, TILE_HEADS * (n + 1))
             q_ps = q_psum.tile([P, TILE_HEADS, HEAD], F32)
             nc.tensor.matmul_mx(

@@ -31,9 +31,10 @@ N_TILE = 512
 TILE_HEADS = N_TILE // HEAD
 A_PASSES = DIM // K_PASS
 B_TILES = HEADS * HEAD // N_TILE
+STEP = 4
 RUN = 4
-A_VECTOR_COLS = 320
-B_VECTOR_COLS = 1280
+A_VECTOR_COLS = (320, 384)
+B_VECTOR_COLS = (192, 512, 128, 0)
 
 FLOPS = 2 * P * DIM * QL + 2 * P * QL * HEADS * HEAD
 
@@ -84,6 +85,10 @@ def tile_mla_pa_s_kernel(tc, x, wq_a, q_norm_w, wq_b, out):
         nc.gpsimd.memset(minus_half[:], -0.5)
         ident = keep.tile([P, P], F32)
         make_identity(nc, ident[:])
+        quarter_turn = keep.tile([P, 1], F32)
+        nc.gpsimd.tensor_scalar(
+            out=quarter_turn[:], in0=minus_half[:], scalar1=-math.pi, scalar2=0.0, op0=ALU.mult, op1=ALU.add
+        )
         warm = keep.tile([P, 1], F32)
         nc.scalar.activation(out=warm[:], in_=minus_half[:], func=ACT.Sin)
 
@@ -95,20 +100,21 @@ def tile_mla_pa_s_kernel(tc, x, wq_a, q_norm_w, wq_b, out):
             out=turns[:, :, 0], in0=position_i[:], scalar1=FIRST_POSITION, scalar2=1.0 / (2.0 * math.pi),
             op0=ALU.add, op1=ALU.mult,
         )
-        w = 1
-        while w < HALF:
+        for j in range(1, STEP):
+            nc.vector.tensor_scalar_mul(out=turns[:, :, j], in0=turns[:, :, 0], scalar1=THETA_1**j)
+        for w in range(STEP, HALF, STEP):
             nc.vector.tensor_scalar_mul(
-                out=turns[:, :, w : 2 * w], in0=turns[:, :, 0:w], scalar1=THETA_1**w
+                out=turns[:, :, w : w + STEP], in0=turns[:, :, 0:STEP], scalar1=THETA_1**w
             )
-            w *= 2
+
         whole = keep.tile([P, HEADS, WRAPPED], I32)
         nc.vector.tensor_copy(out=whole[:], in_=turns[:, :, 0:WRAPPED])
         nc.vector.tensor_tensor(
             out=turns[:, :, 0:WRAPPED], in0=turns[:, :, 0:WRAPPED], in1=whole[:], op=ALU.subtract
         )
-        sin_cos = keep.tile([P, 2, HEADS, HALF], F32)
-        half_sin = keep.tile([P, HEADS, HALF], F32)
-        nc.scalar.activation(out=sin_cos[:, 0], in_=turns[:], func=ACT.Sin, scale=2.0 * math.pi)
+        cos_sin = keep.tile([P, HEADS, 2, HALF], F32)
+        turns_abs = keep.tile([P, HEADS, HALF], F32)
+        nc.scalar.activation(out=turns_abs[:], in_=turns[:], func=ACT.Abs)
 
         x_words = x_sb[:].bitcast(F32)
         xt_ps = psum.tile([P, 2 * A_PASSES, P], F32)
@@ -127,44 +133,62 @@ def tile_mla_pa_s_kernel(tc, x, wq_a, q_norm_w, wq_b, out):
                 out=a_codes[:, g].bitcast(FP8X4), scales=a_scales[:, g], in_=a_grouped[:, g]
             )
 
-        regroup(nc.vector.tensor_copy, a_grouped[:, 0], raw_a[0], 0, A_VECTOR_COLS)
-        regroup(nc.scalar.copy, a_grouped[:, 0], raw_a[0], A_VECTOR_COLS, QL)
+        regroup(nc.vector.tensor_copy, a_grouped[:, 0], raw_a[0], 0, A_VECTOR_COLS[0])
+        regroup(nc.scalar.copy, a_grouped[:, 0], raw_a[0], A_VECTOR_COLS[0], QL)
         quantise_a(0)
+        nc.scalar.activation(out=cos_sin[:, :, 1], in_=turns[:], func=ACT.Sin, scale=2.0 * math.pi)
         nc.scalar.copy(
             out=x_grouped[:].bitcast(F32).rearrange("q (g s u) -> q g s u", g=A_PASSES, u=2),
             in_=xt_ps[:].rearrange("q (g u) s -> q g s u", g=A_PASSES),
         )
-        regroup(nc.vector.tensor_copy, a_grouped[:, 1], raw_a[1], 0, A_VECTOR_COLS)
-        regroup(nc.scalar.copy, a_grouped[:, 1], raw_a[1], A_VECTOR_COLS, QL)
+        regroup(nc.vector.tensor_copy, a_grouped[:, 1], raw_a[1], 0, A_VECTOR_COLS[1])
+        regroup(nc.scalar.copy, a_grouped[:, 1], raw_a[1], A_VECTOR_COLS[1], QL)
         nc.vector.quantize_mx(out=x_codes[:].bitcast(FP8X4), scales=x_scales[:], in_=x_grouped[:])
         quantise_a(1)
 
-        nc.scalar.activation(out=half_sin[:], in_=turns[:], func=ACT.Sin, scale=math.pi)
+
+        def x_op(g):
+            cols = slice(P * g, P * (g + 1))
+            return x_codes[:, cols].bitcast(FP8X4), x_scales[:, cols]
+
+        def a_op(g, cols):
+            return a_codes[:, g, cols].bitcast(FP8X4), a_scales[:, g, cols]
+
+        def multiply_a(out, lhs, rhs, g):
+            nc.tensor.matmul_mx(
+                out=out, lhsT=lhs[0], lhsT_scale=lhs[1], rhs=rhs[0], rhs_scale=rhs[1],
+                start=(g == 0), stop=(g == A_PASSES - 1),
+            )
 
         c_ps = psum.tile([P, QL], F32)
         for g in range(A_PASSES):
-            nc.tensor.matmul_mx(
-                out=c_ps[:],
-                lhsT=x_codes[:, P * g : P * (g + 1)].bitcast(FP8X4),
-                lhsT_scale=x_scales[:, P * g : P * (g + 1)],
-                rhs=a_codes[:, g].bitcast(FP8X4),
-                rhs_scale=a_scales[:, g],
-                start=(g == 0),
-                stop=(g == A_PASSES - 1),
-            )
+            multiply_a(c_ps[:], x_op(g), a_op(g, slice(0, QL)), g)
+        ct_ps = psum.tile([P, PACK, P], F32)
+        for t in range(PACK):
+            for g in range(A_PASSES):
+                multiply_a(ct_ps[:, t, :], a_op(g, slice(P * t, P * (t + 1))), x_op(g), g)
 
         b_grouped = keep.tile([P, B_TILES, PACK * N_TILE], BF16, align_bytes=64)
         b_codes = keep.tile([P, B_TILES, N_TILE], U32, align_bytes=64)
         b_scales = keep.tile([P, B_TILES, N_TILE], U8, align_bytes=64)
 
         def vector_cols(n):
-            return min(max(B_VECTOR_COLS - N_TILE * n, 0), N_TILE)
+            return B_VECTOR_COLS[n]
+
+        def vector_regroup_b(n):
+            if vector_cols(n) > 0:
+                regroup(nc.vector.tensor_copy, b_grouped[:, n], raw_b[n], 0, vector_cols(n))
+
+        def scalar_regroup_b(n):
+            if vector_cols(n) < N_TILE:
+                regroup(nc.scalar.copy, b_grouped[:, n], raw_b[n], vector_cols(n), N_TILE)
 
         def quantise_b(n):
             nc.vector.quantize_mx(
                 out=b_codes[:, n].bitcast(FP8X4), scales=b_scales[:, n], in_=b_grouped[:, n]
             )
 
+        scalar_regroup_b(0)
         squares = keep.tile([P, QL], F32)
         sum_squares = keep.tile([P, 1], F32)
         nc.scalar.activation(out=squares[:], in_=c_ps[:], func=ACT.Square, accum_out=sum_squares[:])
@@ -174,33 +198,27 @@ def tile_mla_pa_s_kernel(tc, x, wq_a, q_norm_w, wq_b, out):
         )
         inv_rms = keep.tile([P, 1], F32)
         nc.gpsimd.tensor_tensor(out=inv_rms[:], in0=mean_square[:], in1=minus_half[:], op=ALU.pow)
-        nc.scalar.activation(out=half_sin[:], in_=half_sin[:], func=ACT.Square)
-        own = [n for n in range(B_TILES) if vector_cols(n) == N_TILE]
-        for n in range(B_TILES):
-            if vector_cols(n) > 0:
-                regroup(nc.vector.tensor_copy, b_grouped[:, n], raw_b[n], 0, vector_cols(n))
-            if n - 1 in own:
-                quantise_b(n - 1)
-        c_scaled = keep.tile([P, QL], F32)
-        ct_ps = psum.tile([P, PACK, P], F32)
-        for half in range(2):
-            cols = slice(QL // 2 * half, QL // 2 * (half + 1))
-            nc.scalar.activation(
-                out=c_scaled[:, cols], in_=c_ps[:, cols], func=ACT.Copy, scale=inv_rms[:, 0:1]
-            )
-            for t in range(PACK // 2 * half, PACK // 2 * (half + 1)):
-                nc.tensor.transpose(ct_ps[:, t, :], c_scaled[:, P * t : P * (t + 1)], ident[:])
-        nc.gpsimd.tensor_scalar(
-            out=sin_cos[:, 1], in0=half_sin[:], scalar1=-2.0, scalar2=1.0, op0=ALU.mult, op1=ALU.add
+        inv_ps = psum.tile([P, P], F32)
+        nc.tensor.transpose(inv_ps[:], inv_rms[:, 0:1].to_broadcast([P, P]), ident[:])
+        nc.scalar.activation(
+            out=cos_sin[:, :, 0], in_=turns_abs[:], func=ACT.Sin, scale=-2.0 * math.pi, bias=quarter_turn[:, 0:1]
         )
-        for n in range(B_TILES):
-            if vector_cols(n) < N_TILE:
-                regroup(nc.scalar.copy, b_grouped[:, n], raw_b[n], vector_cols(n), N_TILE)
+        for n in range(1, B_TILES):
+            scalar_regroup_b(n)
+
+        vector_regroup_b(0)
+        vector_regroup_b(1)
+        quantise_b(0)
+        c_gained = keep.tile([P, PACK, P], F32)
+        nc.vector.tensor_tensor(
+            out=c_gained[:], in0=ct_ps[:], in1=gain[:].unsqueeze(2).to_broadcast([P, PACK, P]), op=ALU.mult
+        )
+        vector_regroup_b(2)
         cn_grouped = keep.tile([P, P, PACK], BF16, align_bytes=64)
         nc.vector.tensor_tensor(
             out=cn_grouped[:],
-            in0=ct_ps[:].rearrange("p t s -> p s t"),
-            in1=gain[:].unsqueeze(1).to_broadcast([P, P, PACK]),
+            in0=c_gained[:].rearrange("p t s -> p s t"),
+            in1=inv_ps[:].unsqueeze(2).to_broadcast([P, P, PACK]),
             op=ALU.mult,
         )
         cn_codes = keep.tile([P, P], U32, align_bytes=64)
@@ -210,13 +228,12 @@ def tile_mla_pa_s_kernel(tc, x, wq_a, q_norm_w, wq_b, out):
             scales=cn_scales[:],
             in_=cn_grouped[:].rearrange("p s t -> p (s t)"),
         )
+        quantise_b(1)
+        quantise_b(2)
 
         out_sb = keep.tile([P, HEADS, HEAD], F32)
         out_rows = out.rearrange("b s h d -> (b s) h d")
-        late = [n for n in range(B_TILES) if n not in own]
         for n in range(B_TILES):
-            if n % 2 == 0 and n // 2 < len(late):
-                quantise_b(late[n // 2])
             heads = slice(TILE_HEADS * n, TILE_HEADS * (n + 1))
             q_ps = q_psum.tile([P, TILE_HEADS, HEAD], F32)
             nc.tensor.matmul_mx(
@@ -228,26 +245,25 @@ def tile_mla_pa_s_kernel(tc, x, wq_a, q_norm_w, wq_b, out):
                 start=True,
                 stop=True,
             )
-            sin = sin_cos[:, 0, heads, :]
-            cos = sin_cos[:, 1, heads, :]
-            rotated = out_sb[:, heads, NOPE:HEAD]
+            products = work.tile([P, TILE_HEADS, 2, 2, HALF], F32)
             nc.vector.tensor_tensor(
-                out=rotated.rearrange("p h (f j) -> p h f j", f=2),
-                in0=q_ps[:, :, NOPE:HEAD].rearrange("p h (f j) -> p h f j", f=2),
-                in1=cos.unsqueeze(2).to_broadcast([P, TILE_HEADS, 2, HALF]),
+                out=products[:],
+                in0=q_ps[:, :, NOPE:HEAD]
+                .rearrange("p h (f j) -> p h f j", f=2)
+                .unsqueeze(2)
+                .to_broadcast([P, TILE_HEADS, 2, 2, HALF]),
+                in1=cos_sin[:, heads].unsqueeze(3).to_broadcast([P, TILE_HEADS, 2, 2, HALF]),
                 op=ALU.mult,
-            )
-            cross = work.tile([P, TILE_HEADS, 2, HALF], F32)
-            nc.vector.scalar_tensor_tensor(
-                out=cross[:, :, 0, :], in0=q_ps[:, :, NOPE + HALF : HEAD], scalar=-1.0, in1=sin,
-                op0=ALU.mult, op1=ALU.mult,
-            )
-            nc.vector.tensor_tensor(
-                out=cross[:, :, 1, :], in0=q_ps[:, :, NOPE : NOPE + HALF], in1=sin, op=ALU.mult
             )
             nc.scalar.copy(out=out_sb[:, heads, 0:NOPE], in_=q_ps[:, :, 0:NOPE])
             adder = nc.gpsimd if n + 1 < B_TILES else nc.vector
-            adder.tensor_tensor(
-                out=rotated, in0=rotated, in1=cross[:].rearrange("p h f j -> p h (f j)"), op=ALU.add
-            )
+            for f, op in ((0, ALU.subtract), (1, ALU.add)):
+                adder.tensor_tensor(
+                    out=out_sb[:, heads, NOPE + HALF * f : NOPE + HALF * (f + 1)],
+                    in0=products[:, :, 0, f, :],
+                    in1=products[:, :, 1, 1 - f, :],
+                    op=op,
+                )
+            if n == 1:
+                quantise_b(3)
             nc.sync.dma_start(out=out_rows[:, heads, :], in_=out_sb[:, heads, :])

@@ -33,8 +33,9 @@ A_PASSES = DIM // K_PASS
 B_TILES = HEADS * HEAD // N_TILE
 STEP = 4
 RUN = 4
-A_VECTOR_COLS = (320, 384)
-B_VECTOR_COLS = (192, 512, 128, 0)
+A_VECTOR_COLS = (384, 384)
+TENSOR_COLS = 256
+B_VECTOR_COLS = (128, 448, 64, 0)
 
 FLOPS = 2 * P * DIM * QL + 2 * P * QL * HEADS * HEAD
 
@@ -50,7 +51,7 @@ def tile_mla_pa_s_kernel(tc, x, wq_a, q_norm_w, wq_b, out):
     nc = tc.nc
     with ExitStack() as ctx:
         keep = ctx.enter_context(tc.tile_pool(name="keep", bufs=1))
-        work = ctx.enter_context(tc.tile_pool(name="work", bufs=2))
+        work = ctx.enter_context(tc.tile_pool(name="work", bufs=3))
         psum = ctx.enter_context(tc.psum_pool(name="psum", bufs=1))
         q_psum = ctx.enter_context(tc.psum_pool(name="q_psum", bufs=B_TILES))
         ctx.enter_context(tc.manual_schedule())
@@ -85,6 +86,8 @@ def tile_mla_pa_s_kernel(tc, x, wq_a, q_norm_w, wq_b, out):
         nc.gpsimd.memset(minus_half[:], -0.5)
         ident = keep.tile([P, P], F32)
         make_identity(nc, ident[:])
+        ident_bf = keep.tile([P, P], BF16)
+        nc.gpsimd.tensor_copy(out=ident_bf[:], in_=ident[:])
         quarter_turn = keep.tile([P, 1], F32)
         nc.gpsimd.tensor_scalar(
             out=quarter_turn[:], in0=minus_half[:], scalar1=-math.pi, scalar2=0.0, op0=ALU.mult, op1=ALU.add
@@ -102,22 +105,32 @@ def tile_mla_pa_s_kernel(tc, x, wq_a, q_norm_w, wq_b, out):
         )
         for j in range(1, STEP):
             nc.vector.tensor_scalar_mul(out=turns[:, :, j], in0=turns[:, :, 0], scalar1=THETA_1**j)
-        for w in range(STEP, HALF, STEP):
+        for w in (*range(WRAPPED, HALF, STEP), *range(STEP, WRAPPED, STEP)):
             nc.vector.tensor_scalar_mul(
                 out=turns[:, :, w : w + STEP], in0=turns[:, :, 0:STEP], scalar1=THETA_1**w
             )
-
         whole = keep.tile([P, HEADS, WRAPPED], I32)
         nc.vector.tensor_copy(out=whole[:], in_=turns[:, :, 0:WRAPPED])
+        wrapped = keep.tile([P, HEADS, WRAPPED], F32)
         nc.vector.tensor_tensor(
-            out=turns[:, :, 0:WRAPPED], in0=turns[:, :, 0:WRAPPED], in1=whole[:], op=ALU.subtract
+            out=wrapped[:], in0=turns[:, :, 0:WRAPPED], in1=whole[:], op=ALU.subtract
         )
         cos_sin = keep.tile([P, HEADS, 2, HALF], F32)
-        turns_abs = keep.tile([P, HEADS, HALF], F32)
-        nc.scalar.activation(out=turns_abs[:], in_=turns[:], func=ACT.Abs)
+        wrapped_abs = keep.tile([P, HEADS, WRAPPED], F32)
+
+        def sine(out, angle):
+            nc.scalar.activation(out=out, in_=angle, func=ACT.Sin, scale=2.0 * math.pi)
+
+        def cosine(out, angle):
+            nc.scalar.activation(
+                out=out, in_=angle, func=ACT.Sin, scale=-2.0 * math.pi, bias=quarter_turn[:, 0:1]
+            )
+
+        sine(cos_sin[:, :, 1, WRAPPED:HALF], turns[:, :, WRAPPED:HALF])
+        cosine(cos_sin[:, :, 0, WRAPPED:HALF], turns[:, :, WRAPPED:HALF])
 
         x_words = x_sb[:].bitcast(F32)
-        xt_ps = psum.tile([P, 2 * A_PASSES, P], F32)
+        xt_ps = psum.tile([P, 2 * A_PASSES, P], F32, name="spare_bank")
         for v in range(2 * A_PASSES):
             nc.tensor.transpose(xt_ps[:, v, :], x_words[:, P * v : P * (v + 1)], ident[:])
         x_grouped = keep.tile([P, A_PASSES * P * PACK], BF16, align_bytes=64)
@@ -136,7 +149,8 @@ def tile_mla_pa_s_kernel(tc, x, wq_a, q_norm_w, wq_b, out):
         regroup(nc.vector.tensor_copy, a_grouped[:, 0], raw_a[0], 0, A_VECTOR_COLS[0])
         regroup(nc.scalar.copy, a_grouped[:, 0], raw_a[0], A_VECTOR_COLS[0], QL)
         quantise_a(0)
-        nc.scalar.activation(out=cos_sin[:, :, 1], in_=turns[:], func=ACT.Sin, scale=2.0 * math.pi)
+        sine(cos_sin[:, :, 1, 0:WRAPPED], wrapped[:])
+        nc.scalar.activation(out=wrapped_abs[:], in_=wrapped[:], func=ACT.Abs)
         nc.scalar.copy(
             out=x_grouped[:].bitcast(F32).rearrange("q (g s u) -> q g s u", g=A_PASSES, u=2),
             in_=xt_ps[:].rearrange("q (g u) s -> q g s u", g=A_PASSES),
@@ -180,14 +194,16 @@ def tile_mla_pa_s_kernel(tc, x, wq_a, q_norm_w, wq_b, out):
                 regroup(nc.vector.tensor_copy, b_grouped[:, n], raw_b[n], 0, vector_cols(n))
 
         def scalar_regroup_b(n):
-            if vector_cols(n) < N_TILE:
-                regroup(nc.scalar.copy, b_grouped[:, n], raw_b[n], vector_cols(n), N_TILE)
+            hi = N_TILE if n + 1 < B_TILES else N_TILE - TENSOR_COLS
+            if vector_cols(n) < hi:
+                regroup(nc.scalar.copy, b_grouped[:, n], raw_b[n], vector_cols(n), hi)
 
         def quantise_b(n):
             nc.vector.quantize_mx(
                 out=b_codes[:, n].bitcast(FP8X4), scales=b_scales[:, n], in_=b_grouped[:, n]
             )
 
+        cosine(cos_sin[:, :, 0, 0:WRAPPED], wrapped_abs[:])
         scalar_regroup_b(0)
         squares = keep.tile([P, QL], F32)
         sum_squares = keep.tile([P, 1], F32)
@@ -200,11 +216,22 @@ def tile_mla_pa_s_kernel(tc, x, wq_a, q_norm_w, wq_b, out):
         nc.gpsimd.tensor_tensor(out=inv_rms[:], in0=mean_square[:], in1=minus_half[:], op=ALU.pow)
         inv_ps = psum.tile([P, P], F32)
         nc.tensor.transpose(inv_ps[:], inv_rms[:, 0:1].to_broadcast([P, P]), ident[:])
-        nc.scalar.activation(
-            out=cos_sin[:, :, 0], in_=turns_abs[:], func=ACT.Sin, scale=-2.0 * math.pi, bias=quarter_turn[:, 0:1]
-        )
+        b_ps = psum.tile([P, TENSOR_COLS, PACK], BF16, name="spare_bank")
+        for part in range(2):
+            w = slice(TENSOR_COLS // 2 * part, TENSOR_COLS // 2 * (part + 1))
+            nc.tensor.matmul(
+                b_ps[:, w, :],
+                lhsT=ident_bf[:],
+                rhs=raw_b[B_TILES - 1][:, :, N_TILE - TENSOR_COLS : N_TILE][:, :, w].rearrange("p t c -> p c t"),
+                start=True,
+                stop=True,
+            )
         for n in range(1, B_TILES):
             scalar_regroup_b(n)
+        nc.scalar.copy(
+            out=b_grouped[:, B_TILES - 1, PACK * (N_TILE - TENSOR_COLS) : PACK * N_TILE],
+            in_=b_ps[:].rearrange("p c t -> p (c t)"),
+        )
 
         vector_regroup_b(0)
         vector_regroup_b(1)
@@ -214,6 +241,7 @@ def tile_mla_pa_s_kernel(tc, x, wq_a, q_norm_w, wq_b, out):
             out=c_gained[:], in0=ct_ps[:], in1=gain[:].unsqueeze(2).to_broadcast([P, PACK, P]), op=ALU.mult
         )
         vector_regroup_b(2)
+        quantise_b(1)
         cn_grouped = keep.tile([P, P, PACK], BF16, align_bytes=64)
         nc.vector.tensor_tensor(
             out=cn_grouped[:],
@@ -228,13 +256,41 @@ def tile_mla_pa_s_kernel(tc, x, wq_a, q_norm_w, wq_b, out):
             scales=cn_scales[:],
             in_=cn_grouped[:].rearrange("p s t -> p (s t)"),
         )
-        quantise_b(1)
         quantise_b(2)
 
         out_sb = keep.tile([P, HEADS, HEAD], F32)
         out_rows = out.rearrange("b s h d -> (b s) h d")
-        for n in range(B_TILES):
+
+        def copy_plain(n, q_ps):
             heads = slice(TILE_HEADS * n, TILE_HEADS * (n + 1))
+            nc.scalar.copy(out=out_sb[:, heads, 0:NOPE], in_=q_ps[:, :, 0:NOPE])
+
+        def multiply_rope(q_ps, first, count, h):
+            products = work.tile([P, count, 2, 2, HALF], F32, name="products%d" % count)
+            nc.vector.tensor_tensor(
+                out=products[:],
+                in0=q_ps[:, h : h + count, NOPE:HEAD]
+                .rearrange("p h (f j) -> p h f j", f=2)
+                .unsqueeze(2)
+                .to_broadcast([P, count, 2, 2, HALF]),
+                in1=cos_sin[:, first : first + count].unsqueeze(3).to_broadcast([P, count, 2, 2, HALF]),
+                op=ALU.mult,
+            )
+            return products
+
+        def add_and_store(adder, products, first, count):
+            heads = slice(first, first + count)
+            for f, op in ((0, ALU.subtract), (1, ALU.add)):
+                adder.tensor_tensor(
+                    out=out_sb[:, heads, NOPE + HALF * f : NOPE + HALF * (f + 1)],
+                    in0=products[:, :, 0, f, :],
+                    in1=products[:, :, 1, 1 - f, :],
+                    op=op,
+                )
+            nc.sync.dma_start(out=out_rows[:, heads, :], in_=out_sb[:, heads, :])
+
+        for n in range(B_TILES):
+            first = TILE_HEADS * n
             q_ps = q_psum.tile([P, TILE_HEADS, HEAD], F32)
             nc.tensor.matmul_mx(
                 out=q_ps[:].rearrange("p h d -> p (h d)"),
@@ -245,25 +301,18 @@ def tile_mla_pa_s_kernel(tc, x, wq_a, q_norm_w, wq_b, out):
                 start=True,
                 stop=True,
             )
-            products = work.tile([P, TILE_HEADS, 2, 2, HALF], F32)
-            nc.vector.tensor_tensor(
-                out=products[:],
-                in0=q_ps[:, :, NOPE:HEAD]
-                .rearrange("p h (f j) -> p h f j", f=2)
-                .unsqueeze(2)
-                .to_broadcast([P, TILE_HEADS, 2, 2, HALF]),
-                in1=cos_sin[:, heads].unsqueeze(3).to_broadcast([P, TILE_HEADS, 2, 2, HALF]),
-                op=ALU.mult,
-            )
-            nc.scalar.copy(out=out_sb[:, heads, 0:NOPE], in_=q_ps[:, :, 0:NOPE])
-            adder = nc.gpsimd if n + 1 < B_TILES else nc.vector
-            for f, op in ((0, ALU.subtract), (1, ALU.add)):
-                adder.tensor_tensor(
-                    out=out_sb[:, heads, NOPE + HALF * f : NOPE + HALF * (f + 1)],
-                    in0=products[:, :, 0, f, :],
-                    in1=products[:, :, 1, 1 - f, :],
-                    op=op,
-                )
+            if n < 2:
+                products = multiply_rope(q_ps, first, TILE_HEADS, 0)
+                copy_plain(n, q_ps)
+                add_and_store(nc.gpsimd, products, first, TILE_HEADS)
+            elif n + 1 < B_TILES:
+                copy_plain(n, q_ps)
+                products = multiply_rope(q_ps, first, TILE_HEADS, 0)
+                add_and_store(nc.gpsimd, products, first, TILE_HEADS)
+            else:
+                copy_plain(n, q_ps)
+                halves = [multiply_rope(q_ps, first + h, TILE_HEADS // 2, h) for h in (0, TILE_HEADS // 2)]
+                for i in range(2):
+                    add_and_store(nc.vector, halves[i], first + TILE_HEADS // 2 * i, TILE_HEADS // 2)
             if n == 1:
                 quantise_b(3)
-            nc.sync.dma_start(out=out_rows[:, heads, :], in_=out_sb[:, heads, :])

@@ -34,7 +34,6 @@ B_TILES = HEADS * HEAD // N_TILE
 STEP = 4
 RUN = 4
 A_VECTOR_COLS = (384, 384)
-TENSOR_COLS = 256
 B_VECTOR_COLS = (128, 448, 64, 0)
 
 FLOPS = 2 * P * DIM * QL + 2 * P * QL * HEADS * HEAD
@@ -86,8 +85,6 @@ def tile_mla_pa_s_kernel(tc, x, wq_a, q_norm_w, wq_b, out):
         nc.gpsimd.memset(minus_half[:], -0.5)
         ident = keep.tile([P, P], F32)
         make_identity(nc, ident[:])
-        ident_bf = keep.tile([P, P], BF16)
-        nc.gpsimd.tensor_copy(out=ident_bf[:], in_=ident[:])
         quarter_turn = keep.tile([P, 1], F32)
         nc.gpsimd.tensor_scalar(
             out=quarter_turn[:], in0=minus_half[:], scalar1=-math.pi, scalar2=0.0, op0=ALU.mult, op1=ALU.add
@@ -130,7 +127,7 @@ def tile_mla_pa_s_kernel(tc, x, wq_a, q_norm_w, wq_b, out):
         cosine(cos_sin[:, :, 0, WRAPPED:HALF], turns[:, :, WRAPPED:HALF])
 
         x_words = x_sb[:].bitcast(F32)
-        xt_ps = psum.tile([P, 2 * A_PASSES, P], F32, name="spare_bank")
+        xt_ps = psum.tile([P, 2 * A_PASSES, P], F32)
         for v in range(2 * A_PASSES):
             nc.tensor.transpose(xt_ps[:, v, :], x_words[:, P * v : P * (v + 1)], ident[:])
         x_grouped = keep.tile([P, A_PASSES * P * PACK], BF16, align_bytes=64)
@@ -194,9 +191,8 @@ def tile_mla_pa_s_kernel(tc, x, wq_a, q_norm_w, wq_b, out):
                 regroup(nc.vector.tensor_copy, b_grouped[:, n], raw_b[n], 0, vector_cols(n))
 
         def scalar_regroup_b(n):
-            hi = N_TILE if n + 1 < B_TILES else N_TILE - TENSOR_COLS
-            if vector_cols(n) < hi:
-                regroup(nc.scalar.copy, b_grouped[:, n], raw_b[n], vector_cols(n), hi)
+            if vector_cols(n) < N_TILE:
+                regroup(nc.scalar.copy, b_grouped[:, n], raw_b[n], vector_cols(n), N_TILE)
 
         def quantise_b(n):
             nc.vector.quantize_mx(
@@ -216,22 +212,8 @@ def tile_mla_pa_s_kernel(tc, x, wq_a, q_norm_w, wq_b, out):
         nc.gpsimd.tensor_tensor(out=inv_rms[:], in0=mean_square[:], in1=minus_half[:], op=ALU.pow)
         inv_ps = psum.tile([P, P], F32)
         nc.tensor.transpose(inv_ps[:], inv_rms[:, 0:1].to_broadcast([P, P]), ident[:])
-        b_ps = psum.tile([P, TENSOR_COLS, PACK], BF16, name="spare_bank")
-        for part in range(2):
-            w = slice(TENSOR_COLS // 2 * part, TENSOR_COLS // 2 * (part + 1))
-            nc.tensor.matmul(
-                b_ps[:, w, :],
-                lhsT=ident_bf[:],
-                rhs=raw_b[B_TILES - 1][:, :, N_TILE - TENSOR_COLS : N_TILE][:, :, w].rearrange("p t c -> p c t"),
-                start=True,
-                stop=True,
-            )
         for n in range(1, B_TILES):
             scalar_regroup_b(n)
-        nc.scalar.copy(
-            out=b_grouped[:, B_TILES - 1, PACK * (N_TILE - TENSOR_COLS) : PACK * N_TILE],
-            in_=b_ps[:].rearrange("p c t -> p (c t)"),
-        )
 
         vector_regroup_b(0)
         vector_regroup_b(1)

@@ -69,9 +69,9 @@ def tile_mla_pa_s_kernel(tc, x, wq_a, q_norm_w, wq_b, out):
         load_a(0)
         nc.sync.dma_start(out=x_sb[:], in_=x.rearrange("b s k -> (b s) k"))
         load_a(1)
-        gain = keep.tile([P, PACK], BF16)
-        with nc.allow_non_contiguous_dma(reason="512 single values"):
-            nc.sync.dma_start(out=gain[:], in_=q_norm_w.rearrange("(t p) -> p t", p=P))
+        gain_rows = keep.tile([P, P], BF16)
+        nc.gpsimd.memset(gain_rows[:], 0.0)
+        nc.sync.dma_start(out=gain_rows[0:PACK, :], in_=q_norm_w.rearrange("(t p) -> t p", p=P))
         raw_b = [keep.tile([P, PACK, N_TILE], BF16, name="raw_b%d" % n) for n in range(B_TILES)]
         for n in range(B_TILES):
             nc.sync.dma_start(
@@ -123,6 +123,9 @@ def tile_mla_pa_s_kernel(tc, x, wq_a, q_norm_w, wq_b, out):
                 out=out, in_=angle, func=ACT.Sin, scale=-2.0 * math.pi, bias=quarter_turn[:, 0:1]
             )
 
+        ident_bf = keep.tile([P, P], BF16)
+        nc.vector.tensor_copy(out=ident_bf[:], in_=ident[:])
+
         sine(cos_sin[:, :, 1, WRAPPED:HALF], turns[:, :, WRAPPED:HALF])
         cosine(cos_sin[:, :, 0, WRAPPED:HALF], turns[:, :, WRAPPED:HALF])
 
@@ -130,6 +133,9 @@ def tile_mla_pa_s_kernel(tc, x, wq_a, q_norm_w, wq_b, out):
         xt_ps = psum.tile([P, 2 * A_PASSES, P], F32)
         for v in range(2 * A_PASSES):
             nc.tensor.transpose(xt_ps[:, v, :], x_words[:, P * v : P * (v + 1)], ident[:])
+        gain_ps = psum.tile([P, P], BF16, name="small_bank")
+        nc.tensor.transpose(gain_ps[:], gain_rows[:], ident_bf[:])
+        gain = keep.tile([P, PACK], BF16)
         x_grouped = keep.tile([P, A_PASSES * P * PACK], BF16, align_bytes=64)
         x_codes = keep.tile([P, A_PASSES * P], U32, align_bytes=64)
         x_scales = keep.tile([P, A_PASSES * P], U8, align_bytes=64)
@@ -199,6 +205,7 @@ def tile_mla_pa_s_kernel(tc, x, wq_a, q_norm_w, wq_b, out):
                 out=b_codes[:, n].bitcast(FP8X4), scales=b_scales[:, n], in_=b_grouped[:, n]
             )
 
+        nc.scalar.copy(out=gain[:], in_=gain_ps[:, 0:PACK])
         cosine(cos_sin[:, :, 0, 0:WRAPPED], wrapped_abs[:])
         scalar_regroup_b(0)
         squares = keep.tile([P, QL], F32)
@@ -210,7 +217,7 @@ def tile_mla_pa_s_kernel(tc, x, wq_a, q_norm_w, wq_b, out):
         )
         inv_rms = keep.tile([P, 1], F32)
         nc.gpsimd.tensor_tensor(out=inv_rms[:], in0=mean_square[:], in1=minus_half[:], op=ALU.pow)
-        inv_ps = psum.tile([P, P], F32)
+        inv_ps = psum.tile([P, P], F32, name="small_bank")
         nc.tensor.transpose(inv_ps[:], inv_rms[:, 0:1].to_broadcast([P, P]), ident[:])
         for n in range(1, B_TILES):
             scalar_regroup_b(n)

@@ -293,15 +293,16 @@ def tile_mla_pa_s_kernel(tc, x, wq_a, q_norm_w, wq_b, out):
             if n < 2:
                 products = multiply_rope(q_ps, first, TILE_HEADS, 0)
                 copy_plain(n, q_ps)
-                add_and_store(nc.gpsimd, products, first, TILE_HEADS)
             elif n + 1 < B_TILES:
                 copy_plain(n, q_ps)
                 products = multiply_rope(q_ps, first, TILE_HEADS, 0)
-                add_and_store(nc.gpsimd, products, first, TILE_HEADS)
             else:
                 copy_plain(n, q_ps)
                 halves = [multiply_rope(q_ps, first + h, TILE_HEADS // 2, h) for h in (0, TILE_HEADS // 2)]
-                for i in range(2):
-                    add_and_store(nc.vector, halves[i], first + TILE_HEADS // 2 * i, TILE_HEADS // 2)
+            if n > 0:
+                add_and_store(nc.vector, waiting, first - TILE_HEADS, TILE_HEADS)
+            waiting = products
             if n == 1:
                 quantise_b(3)
+        for i in range(2):
+            add_and_store(nc.vector, halves[i], first + TILE_HEADS // 2 * i, TILE_HEADS // 2)

@@ -34,6 +34,8 @@ B_TILES = HEADS * HEAD // N_TILE
 STEP = 4
 RUN = 4
 A_VECTOR_COLS = (384, 384)
+TENSOR_COLS = 256
+TENSOR_RUN = 8
 B_VECTOR_COLS = (128, 448, 64, 0)
 
 FLOPS = 2 * P * DIM * QL + 2 * P * QL * HEADS * HEAD
@@ -130,7 +132,7 @@ def tile_mla_pa_s_kernel(tc, x, wq_a, q_norm_w, wq_b, out):
         cosine(cos_sin[:, :, 0, WRAPPED:HALF], turns[:, :, WRAPPED:HALF])
 
         x_words = x_sb[:].bitcast(F32)
-        xt_ps = psum.tile([P, 2 * A_PASSES, P], F32)
+        xt_ps = psum.tile([P, 2 * A_PASSES, P], F32, name="spare_bank")
         for v in range(2 * A_PASSES):
             nc.tensor.transpose(xt_ps[:, v, :], x_words[:, P * v : P * (v + 1)], ident[:])
         gain_ps = psum.tile([P, P], BF16, name="small_bank")
@@ -197,8 +199,9 @@ def tile_mla_pa_s_kernel(tc, x, wq_a, q_norm_w, wq_b, out):
                 regroup(nc.vector.tensor_copy, b_grouped[:, n], raw_b[n], 0, vector_cols(n))
 
         def scalar_regroup_b(n):
-            if vector_cols(n) < N_TILE:
-                regroup(nc.scalar.copy, b_grouped[:, n], raw_b[n], vector_cols(n), N_TILE)
+            hi = N_TILE if n + 1 < B_TILES else N_TILE - TENSOR_COLS
+            if vector_cols(n) < hi:
+                regroup(nc.scalar.copy, b_grouped[:, n], raw_b[n], vector_cols(n), hi)
 
         def quantise_b(n):
             nc.vector.quantize_mx(
@@ -219,8 +222,24 @@ def tile_mla_pa_s_kernel(tc, x, wq_a, q_norm_w, wq_b, out):
         nc.gpsimd.tensor_tensor(out=inv_rms[:], in0=mean_square[:], in1=minus_half[:], op=ALU.pow)
         inv_ps = psum.tile([P, P], F32, name="small_bank")
         nc.tensor.transpose(inv_ps[:], inv_rms[:, 0:1].to_broadcast([P, P]), ident[:])
+        b_ps = psum.tile([P, TENSOR_COLS * PACK], BF16, name="spare_bank")
+        for part in range(2):
+            lo = N_TILE - TENSOR_COLS + TENSOR_COLS // 2 * part
+            out_cols = slice(TENSOR_COLS // 2 * PACK * part, TENSOR_COLS // 2 * PACK * (part + 1))
+            nc.tensor.matmul(
+                b_ps[:, out_cols].rearrange("p (c i t) -> p c t i", i=TENSOR_RUN, t=PACK),
+                lhsT=ident_bf[:],
+                rhs=raw_b[B_TILES - 1][:, :, lo : lo + TENSOR_COLS // 2].rearrange(
+                    "p t (c i) -> p c t i", i=TENSOR_RUN
+                ),
+                start=True,
+                stop=True,
+            )
         for n in range(1, B_TILES):
             scalar_regroup_b(n)
+        nc.scalar.copy(
+            out=b_grouped[:, B_TILES - 1, PACK * (N_TILE - TENSOR_COLS) : PACK * N_TILE], in_=b_ps[:]
+        )
 
         vector_regroup_b(0)
         vector_regroup_b(1)

@@ -36,7 +36,7 @@ RUN = 4
 A_VECTOR_COLS = (384, 384)
 TENSOR_COLS = 256
 TENSOR_RUN = 8
-B_VECTOR_COLS = (128, 448, 64, 0)
+B_VECTOR_COLS = (256, 384, 64, 0)
 
 FLOPS = 2 * P * DIM * QL + 2 * P * QL * HEADS * HEAD
 
@@ -248,8 +248,8 @@ def tile_mla_pa_s_kernel(tc, x, wq_a, q_norm_w, wq_b, out):
         nc.vector.tensor_tensor(
             out=c_gained[:], in0=ct_ps[:], in1=gain[:].unsqueeze(2).to_broadcast([P, PACK, P]), op=ALU.mult
         )
-        vector_regroup_b(2)
         quantise_b(1)
+        vector_regroup_b(2)
         cn_grouped = keep.tile([P, P, PACK], BF16, align_bytes=64)
         nc.vector.tensor_tensor(
             out=cn_grouped[:],
@@ -318,8 +318,10 @@ def tile_mla_pa_s_kernel(tc, x, wq_a, q_norm_w, wq_b, out):
             else:
                 copy_plain(n, q_ps)
                 halves = [multiply_rope(q_ps, first + h, TILE_HEADS // 2, h) for h in (0, TILE_HEADS // 2)]
-            if n > 0:
+            if 0 < n < B_TILES - 1:
                 add_and_store(nc.vector, waiting, first - TILE_HEADS, TILE_HEADS)
+            if n == B_TILES - 2:
+                add_and_store(nc.vector, products, first, TILE_HEADS)
             waiting = products
             if n == 1:
                 quantise_b(3)

import math
from contextlib import ExitStack

import concourse.mybir as mybir
from concourse.masks import make_identity

F32 = mybir.dt.float32
BF16 = mybir.dt.bfloat16
I32 = mybir.dt.int32
U32 = mybir.dt.uint32
U8 = mybir.dt.uint8
FP8X4 = mybir.dt.float8_e4m3fn_x4
ALU = mybir.AluOpType
ACT = mybir.ActivationFunctionType

P = 128
PACK = 4
K_PASS = P * PACK
DIM = 1024
QL = 512
HEADS = 16
HEAD = 128
NOPE = 64
HALF = 32
FIRST_POSITION = 37
EPS = 1e-6
THETA_1 = 10000.0 ** (-1.0 / HALF)
WRAPPED = 16
assert (P - 1 + FIRST_POSITION) * THETA_1**WRAPPED < math.pi
N_TILE = 512
TILE_HEADS = N_TILE // HEAD
A_PASSES = DIM // K_PASS
B_TILES = HEADS * HEAD // N_TILE
STEP = 4
RUN = 4
A_VECTOR_COLS = (384, 384)
TENSOR_COLS = 256
TENSOR_RUN = 8
B_VECTOR_COLS = (256, 384, 64, 0)

FLOPS = 2 * P * DIM * QL + 2 * P * QL * HEADS * HEAD


def regroup(copy, grouped, raw, lo, hi):
    copy(
        out=grouped[:, PACK * lo : PACK * hi].rearrange("p (c i t) -> p c t i", i=RUN, t=PACK),
        in_=raw[:, :, lo:hi].rearrange("p t (c i) -> p c t i", i=RUN),
    )


def tile_mla_pa_s_kernel(tc, x, wq_a, q_norm_w, wq_b, out):
    nc = tc.nc
    with ExitStack() as ctx:
        keep = ctx.enter_context(tc.tile_pool(name="keep", bufs=1))
        work = ctx.enter_context(tc.tile_pool(name="work", bufs=3))
        psum = ctx.enter_context(tc.psum_pool(name="psum", bufs=1))
        q_psum = ctx.enter_context(tc.psum_pool(name="q_psum", bufs=B_TILES))
        ctx.enter_context(tc.manual_schedule())

        x_sb = keep.tile([P, DIM], BF16)
        raw_a = [keep.tile([P, PACK, QL], BF16, name="raw_a%d" % g) for g in range(A_PASSES)]

        def load_a(g):
            nc.sync.dma_start(
                out=raw_a[g][:].rearrange("q (u e) c -> q u e c", u=2),
                in_=wq_a[K_PASS * g : K_PASS * (g + 1), :].rearrange(
                    "(u q e) c -> q u e c", u=2, e=2
                ),
            )

        load_a(0)
        nc.sync.dma_start(out=x_sb[:], in_=x.rearrange("b s k -> (b s) k"))
        load_a(1)
        gain_rows = keep.tile([P, P], BF16)
        nc.gpsimd.memset(gain_rows[:], 0.0)
        nc.sync.dma_start(out=gain_rows[0:PACK, :], in_=q_norm_w.rearrange("(t p) -> t p", p=P))
        raw_b = [keep.tile([P, PACK, N_TILE], BF16, name="raw_b%d" % n) for n in range(B_TILES)]
        for n in range(B_TILES):
            nc.sync.dma_start(
                out=raw_b[n][:],
                in_=wq_b[:, N_TILE * n : N_TILE * (n + 1)].rearrange("(t p) c -> p t c", p=P),
            )

        position_i = keep.tile([P, HEADS], I32)
        nc.gpsimd.iota(position_i[:], pattern=[[1, HEADS]], base=0, channel_multiplier=HEADS)
        minus_half = keep.tile([P, 1], F32)
        nc.gpsimd.memset(minus_half[:], -0.5)
        ident = keep.tile([P, P], F32)
        make_identity(nc, ident[:])
        quarter_turn = keep.tile([P, 1], F32)
        nc.gpsimd.tensor_scalar(
            out=quarter_turn[:], in0=minus_half[:], scalar1=-math.pi, scalar2=0.0, op0=ALU.mult, op1=ALU.add
        )
        warm = keep.tile([P, 1], F32)
        nc.scalar.activation(out=warm[:], in_=minus_half[:], func=ACT.Sin)

        turns = keep.tile([P, HEADS, HALF], F32)
        nc.vector.tensor_single_scalar(
            out=position_i[:], in_=position_i[:], scalar=P - 1, op=ALU.bitwise_and
        )
        nc.vector.tensor_scalar(
            out=turns[:, :, 0], in0=position_i[:], scalar1=FIRST_POSITION, scalar2=1.0 / (2.0 * math.pi),
            op0=ALU.add, op1=ALU.mult,
        )
        for j in range(1, STEP):
            nc.vector.tensor_scalar_mul(out=turns[:, :, j], in0=turns[:, :, 0], scalar1=THETA_1**j)
        for w in (*range(WRAPPED, HALF, STEP), *range(STEP, WRAPPED, STEP)):
            nc.vector.tensor_scalar_mul(
                out=turns[:, :, w : w + STEP], in0=turns[:, :, 0:STEP], scalar1=THETA_1**w
            )
        whole = keep.tile([P, HEADS, WRAPPED], I32)
        nc.vector.tensor_copy(out=whole[:], in_=turns[:, :, 0:WRAPPED])
        wrapped = keep.tile([P, HEADS, WRAPPED], F32)
        nc.vector.tensor_tensor(
            out=wrapped[:], in0=turns[:, :, 0:WRAPPED], in1=whole[:], op=ALU.subtract
        )
        cos_sin = keep.tile([P, HEADS, 2, HALF], F32)
        wrapped_abs = keep.tile([P, HEADS, WRAPPED], F32)

        def sine(out, angle):
            nc.scalar.activation(out=out, in_=angle, func=ACT.Sin, scale=2.0 * math.pi)

        def cosine(out, angle):
            nc.scalar.activation(
                out=out, in_=angle, func=ACT.Sin, scale=-2.0 * math.pi, bias=quarter_turn[:, 0:1]
            )

        ident_bf = keep.tile([P, P], BF16)
        nc.vector.tensor_copy(out=ident_bf[:], in_=ident[:])

        sine(cos_sin[:, :, 1, WRAPPED:HALF], turns[:, :, WRAPPED:HALF])
        cosine(cos_sin[:, :, 0, WRAPPED:HALF], turns[:, :, WRAPPED:HALF])

        x_words = x_sb[:].bitcast(F32)
        xt_ps = psum.tile([P, 2 * A_PASSES, P], F32, name="spare_bank")
        for v in range(2 * A_PASSES):
            nc.tensor.transpose(xt_ps[:, v, :], x_words[:, P * v : P * (v + 1)], ident[:])
        gain_ps = psum.tile([P, P], BF16, name="small_bank")
        nc.tensor.transpose(gain_ps[:], gain_rows[:], ident_bf[:])
        gain = keep.tile([P, PACK], BF16)
        x_grouped = keep.tile([P, A_PASSES * P * PACK], BF16, align_bytes=64)
        x_codes = keep.tile([P, A_PASSES * P], U32, align_bytes=64)
        x_scales = keep.tile([P, A_PASSES * P], U8, align_bytes=64)

        a_grouped = keep.tile([P, A_PASSES, PACK * QL], BF16, align_bytes=64)
        a_codes = keep.tile([P, A_PASSES, QL], U32, align_bytes=64)
        a_scales = keep.tile([P, A_PASSES, QL], U8, align_bytes=64)

        def quantise_a(g):
            nc.vector.quantize_mx(
                out=a_codes[:, g].bitcast(FP8X4), scales=a_scales[:, g], in_=a_grouped[:, g]
            )

        regroup(nc.vector.tensor_copy, a_grouped[:, 0], raw_a[0], 0, A_VECTOR_COLS[0])
        regroup(nc.scalar.copy, a_grouped[:, 0], raw_a[0], A_VECTOR_COLS[0], QL)
        quantise_a(0)
        sine(cos_sin[:, :, 1, 0:WRAPPED], wrapped[:])
        nc.scalar.activation(out=wrapped_abs[:], in_=wrapped[:], func=ACT.Abs)
        nc.scalar.copy(
            out=x_grouped[:].bitcast(F32).rearrange("q (g s u) -> q g s u", g=A_PASSES, u=2),
            in_=xt_ps[:].rearrange("q (g u) s -> q g s u", g=A_PASSES),
        )
        regroup(nc.vector.tensor_copy, a_grouped[:, 1], raw_a[1], 0, A_VECTOR_COLS[1])
        regroup(nc.scalar.copy, a_grouped[:, 1], raw_a[1], A_VECTOR_COLS[1], QL)
        nc.vector.quantize_mx(out=x_codes[:].bitcast(FP8X4), scales=x_scales[:], in_=x_grouped[:])
        quantise_a(1)


        def x_op(g):
            cols = slice(P * g, P * (g + 1))
            return x_codes[:, cols].bitcast(FP8X4), x_scales[:, cols]

        def a_op(g, cols):
            return a_codes[:, g, cols].bitcast(FP8X4), a_scales[:, g, cols]

        def multiply_a(out, lhs, rhs, g):
            nc.tensor.matmul_mx(
                out=out, lhsT=lhs[0], lhsT_scale=lhs[1], rhs=rhs[0], rhs_scale=rhs[1],
                start=(g == 0), stop=(g == A_PASSES - 1),
            )

        c_ps = psum.tile([P, QL], F32)
        for g in range(A_PASSES):
            multiply_a(c_ps[:], x_op(g), a_op(g, slice(0, QL)), g)
        ct_ps = psum.tile([P, PACK, P], F32)
        for t in range(PACK):
            for g in range(A_PASSES):
                multiply_a(ct_ps[:, t, :], a_op(g, slice(P * t, P * (t + 1))), x_op(g), g)

        b_grouped = keep.tile([P, B_TILES, PACK * N_TILE], BF16, align_bytes=64)
        b_codes = keep.tile([P, B_TILES, N_TILE], U32, align_bytes=64)
        b_scales = keep.tile([P, B_TILES, N_TILE], U8, align_bytes=64)

        def vector_cols(n):
            return B_VECTOR_COLS[n]

        def vector_regroup_b(n):
            if vector_cols(n) > 0:
                regroup(nc.vector.tensor_copy, b_grouped[:, n], raw_b[n], 0, vector_cols(n))

        def scalar_regroup_b(n):
            hi = N_TILE if n + 1 < B_TILES else N_TILE - TENSOR_COLS
            if vector_cols(n) < hi:
                regroup(nc.scalar.copy, b_grouped[:, n], raw_b[n], vector_cols(n), hi)

        def quantise_b(n):
            nc.vector.quantize_mx(
                out=b_codes[:, n].bitcast(FP8X4), scales=b_scales[:, n], in_=b_grouped[:, n]
            )

        nc.scalar.copy(out=gain[:], in_=gain_ps[:, 0:PACK])
        cosine(cos_sin[:, :, 0, 0:WRAPPED], wrapped_abs[:])
        scalar_regroup_b(0)
        squares = keep.tile([P, QL], F32)
        sum_squares = keep.tile([P, 1], F32)
        nc.scalar.activation(out=squares[:], in_=c_ps[:], func=ACT.Square, accum_out=sum_squares[:])
        mean_square = keep.tile([P, 1], F32)
        nc.scalar.activation(
            out=mean_square[:], in_=sum_squares[:], func=ACT.Copy, scale=1.0 / QL, bias=EPS
        )
        inv_rms = keep.tile([P, 1], F32)
        nc.gpsimd.tensor_tensor(out=inv_rms[:], in0=mean_square[:], in1=minus_half[:], op=ALU.pow)
        inv_ps = psum.tile([P, P], F32, name="small_bank")
        nc.tensor.transpose(inv_ps[:], inv_rms[:, 0:1].to_broadcast([P, P]), ident[:])
        b_ps = psum.tile([P, TENSOR_COLS * PACK], BF16, name="spare_bank")
        for part in range(2):
            lo = N_TILE - TENSOR_COLS + TENSOR_COLS // 2 * part
            out_cols = slice(TENSOR_COLS // 2 * PACK * part, TENSOR_COLS // 2 * PACK * (part + 1))
            nc.tensor.matmul(
                b_ps[:, out_cols].rearrange("p (c i t) -> p c t i", i=TENSOR_RUN, t=PACK),
                lhsT=ident_bf[:],
                rhs=raw_b[B_TILES - 1][:, :, lo : lo + TENSOR_COLS // 2].rearrange(
                    "p t (c i) -> p c t i", i=TENSOR_RUN
                ),
                start=True,
                stop=True,
            )
        for n in range(1, B_TILES):
            scalar_regroup_b(n)
        nc.scalar.copy(
            out=b_grouped[:, B_TILES - 1, PACK * (N_TILE - TENSOR_COLS) : PACK * N_TILE], in_=b_ps[:]
        )

        vector_regroup_b(0)
        vector_regroup_b(1)
        quantise_b(0)
        c_gained = keep.tile([P, PACK, P], F32)
        nc.vector.tensor_tensor(
            out=c_gained[:], in0=ct_ps[:], in1=gain[:].unsqueeze(2).to_broadcast([P, PACK, P]), op=ALU.mult
        )
        quantise_b(1)
        vector_regroup_b(2)
        cn_grouped = keep.tile([P, P, PACK], BF16, align_bytes=64)
        nc.vector.tensor_tensor(
            out=cn_grouped[:],
            in0=c_gained[:].rearrange("p t s -> p s t"),
            in1=inv_ps[:].unsqueeze(2).to_broadcast([P, P, PACK]),
            op=ALU.mult,
        )
        cn_codes = keep.tile([P, P], U32, align_bytes=64)
        cn_scales = keep.tile([P, P], U8, align_bytes=64)
        nc.vector.quantize_mx(
            out=cn_codes[:].bitcast(FP8X4),
            scales=cn_scales[:],
            in_=cn_grouped[:].rearrange("p s t -> p (s t)"),
        )
        quantise_b(2)

        out_sb = keep.tile([P, HEADS, HEAD], F32)
        out_rows = out.rearrange("b s h d -> (b s) h d")

        def copy_plain(n, q_ps):
            heads = slice(TILE_HEADS * n, TILE_HEADS * (n + 1))
            nc.scalar.copy(out=out_sb[:, heads, 0:NOPE], in_=q_ps[:, :, 0:NOPE])

        def multiply_rope(q_ps, first, count, h):
            products = work.tile([P, count, 2, 2, HALF], F32, name="products%d" % count)
            nc.vector.tensor_tensor(
                out=products[:],
                in0=q_ps[:, h : h + count, NOPE:HEAD]
                .rearrange("p h (f j) -> p h f j", f=2)
                .unsqueeze(2)
                .to_broadcast([P, count, 2, 2, HALF]),
                in1=cos_sin[:, first : first + count].unsqueeze(3).to_broadcast([P, count, 2, 2, HALF]),
                op=ALU.mult,
            )
            return products

        def add_and_store(adder, products, first, count):
            heads = slice(first, first + count)
            for f, op in ((0, ALU.subtract), (1, ALU.add)):
                adder.tensor_tensor(
                    out=out_sb[:, heads, NOPE + HALF * f : NOPE + HALF * (f + 1)],
                    in0=products[:, :, 0, f, :],
                    in1=products[:, :, 1, 1 - f, :],
                    op=op,
                )
            nc.sync.dma_start(out=out_rows[:, heads, :], in_=out_sb[:, heads, :])

        for n in range(B_TILES):
            first = TILE_HEADS * n
            q_ps = q_psum.tile([P, TILE_HEADS, HEAD], F32)
            nc.tensor.matmul_mx(
                out=q_ps[:].rearrange("p h d -> p (h d)"),
                lhsT=cn_codes[:].bitcast(FP8X4),
                lhsT_scale=cn_scales[:],
                rhs=b_codes[:, n].bitcast(FP8X4),
                rhs_scale=b_scales[:, n],
                start=True,
                stop=True,
            )
            if n < 2:
                products = multiply_rope(q_ps, first, TILE_HEADS, 0)
                copy_plain(n, q_ps)
            elif n + 1 < B_TILES:
                copy_plain(n, q_ps)
                products = multiply_rope(q_ps, first, TILE_HEADS, 0)
            else:
                copy_plain(n, q_ps)
                halves = [multiply_rope(q_ps, first + h, TILE_HEADS // 2, h) for h in (0, TILE_HEADS // 2)]
            if 0 < n < B_TILES - 1:
                add_and_store(nc.vector, waiting, first - TILE_HEADS, TILE_HEADS)
            if n == B_TILES - 2:
                add_and_store(nc.vector, products, first, TILE_HEADS)
            waiting = products
            if n == 1:
                quantise_b(3)
        for i in range(2):
            add_and_store(nc.vector, halves[i], first + TILE_HEADS // 2 * i, TILE_HEADS // 2)
